import numpy as np
import ml_dtypes

BF16 = ml_dtypes.bfloat16


def bf(x):
    return np.asarray(x, np.float32).astype(BF16)


def f32(x):
    return np.asarray(x, np.float32)


def f64(x):
    return np.asarray(x).astype(np.float64)


def striped(idx):
    return np.tile(idx.reshape(-1, 16).T, (8, 1))


V, D, T, B, NH, DH, N = 1024, 512, 256, 8, 4, 128, 2048
EPS = 1e-5
BASE = 10000.0


def pos_table():
    i = np.arange(D)
    const = f32(BASE ** (f64(np.where(i % 2 == 0, i, i - 1)) / D))
    ang = f32(np.arange(T))[None, :] / const[:, None]
    return np.where((i % 2 == 0)[:, None], np.sin(f64(ang)), np.cos(f64(ang)))


def setup_inputs():
    return {"emb": f32(np.random.standard_normal((D, V))), "pos": f32(pos_table()), "wq": bf(np.random.standard_normal((D, D)) / np.sqrt(D)), "wk": bf(np.random.standard_normal((D, D)) / np.sqrt(D)), "wv": bf(np.random.standard_normal((D, D)) / np.sqrt(D)), "wp": bf(np.random.standard_normal((D, D)) / np.sqrt(D)), "ln_w": f32(1.0 + 0.1 * np.random.standard_normal((D, 1))), "ln_b": f32(0.1 * np.random.standard_normal((D, 1))), "offs": striped(np.random.permutation(np.tile(np.arange(V), 2))[:N])}


def reference(emb, pos, wq, wk, wv, wp, ln_w, ln_b, offs):
    idx = offs[:16].T.reshape(-1)
    h = f64(emb)[:, idx] + np.tile(f64(pos), (1, B))
    q = (f64(wq).T @ h).reshape(NH, DH, B, T)
    k = (f64(wk).T @ h).reshape(NH, DH, B, T)
    v = (f64(wv).T @ h).reshape(NH, DH, B, T)
    sc = np.einsum("hdbq,hdbk->bhqk", q, k) / np.sqrt(DH)
    sc = np.where(np.arange(T)[None, :] > np.arange(T)[:, None], -np.inf, sc)
    e = np.exp(sc - sc.max(-1, keepdims=True))
    a = e / e.sum(-1, keepdims=True)
    o = np.einsum("bhqk,hdbk->hdbq", a, v).reshape(D, N)
    r = h + f64(wp).T @ o
    m = r.mean(0, keepdims=True)
    var = ((r - m) ** 2).mean(0, keepdims=True)
    return (r - m) / np.sqrt(var + EPS) * f64(ln_w) + f64(ln_b)

@@ -1,0 +1,254 @@
+import math
+
+import concourse.mybir as mybir
+from concourse.masks import make_identity
+
+F32 = mybir.dt.float32
+BF16 = mybir.dt.bfloat16
+U16 = mybir.dt.uint16
+I32 = mybir.dt.int32
+ALU = mybir.AluOpType
+ACT = mybir.ActivationFunctionType
+AXIS = mybir.AxisListType
+
+P = 128
+VOCAB, D, T, SEQS, HEADS = 1024, 512, 256, 8, 4
+N = SEQS * T
+BLOCKS = D // P
+BANK = 512
+CHUNKS = N // BANK
+SCALE = 1.0 / math.sqrt(P)
+EPS = 1e-5
+MASKED = -1e30
+
+FLOPS = 4 * 2 * D * D * N + 2 * 2 * SEQS * HEADS * P * (T * (T + 1) // 2)
+
+
+def tile_first_decoder_b_kernel(tc, emb, pos, wq, wk, wv, wp, ln_w, ln_b, offs, out):
+    nc = tc.nc
+    with (
+        tc.tile_pool(name="held", bufs=1) as held,
+        tc.tile_pool(name="soft", bufs=4) as soft,
+        tc.tile_pool(name="norm", bufs=8) as norm,
+        tc.psum_pool(name="banks", bufs=8) as banks,
+    ):
+        offsets = held.tile([P, N // 16], U16, name="offsets")
+        nc.sync.dma_start(offsets[:], offs)
+        pos_sb = held.tile([P, BLOCKS, T], F32, name="pos_sb")
+        nc.scalar.dma_start(pos_sb[:], pos.rearrange("(c p) t -> p c t", p=P))
+        emb_sb = [held.tile([P, VOCAB], F32, name=f"emb_sb{c}") for c in range(BLOCKS)]
+        for c in range(BLOCKS):
+            queue = nc.sync if c % 2 == 0 else nc.scalar
+            queue.dma_start(emb_sb[c][:], emb[c * P : (c + 1) * P, :])
+        wq_sb = held.tile([P, BLOCKS, D], BF16, name="wq_sb")
+        wk_sb = held.tile([P, BLOCKS, D], BF16, name="wk_sb")
+        wv_sb = held.tile([P, BLOCKS, D], BF16, name="wv_sb")
+        wp_sb = held.tile([P, BLOCKS, D], BF16, name="wp_sb")
+        nc.sync.dma_start(wq_sb[:], wq.rearrange("(c p) e -> p c e", p=P))
+        nc.scalar.dma_start(wk_sb[:], wk.rearrange("(c p) e -> p c e", p=P))
+        nc.sync.dma_start(wv_sb[:], wv.rearrange("(c p) e -> p c e", p=P))
+        nc.scalar.dma_start(wp_sb[:], wp.rearrange("(c p) e -> p c e", p=P))
+        ln_rows = held.tile([2 * BLOCKS, P], F32, name="ln_rows")
+        nc.gpsimd.dma_start(ln_rows[0:BLOCKS, :], ln_w.rearrange("(c p) o -> c (p o)", p=P))
+        nc.gpsimd.dma_start(ln_rows[BLOCKS : 2 * BLOCKS, :], ln_b.rearrange("(c p) o -> c (p o)", p=P))
+
+        ident16 = held.tile([P, P], BF16, name="ident16")
+        make_identity(nc, ident16[:])
+        ident32 = held.tile([P, P], F32, name="ident32")
+        make_identity(nc, ident32[:])
+        ahead = held.tile([P, HEADS * P], I32, name="ahead")
+        nc.gpsimd.iota(ahead[:], pattern=[[0, HEADS], [1, P]], base=0, channel_multiplier=-1)
+        mask = held.tile([P, HEADS * P], BF16, name="mask")
+        nc.vector.tensor_scalar(mask[:], ahead[:], 0.0, MASKED, ALU.is_gt, ALU.mult)
+        neg_half = held.tile([P, 1], F32, name="neg_half")
+        nc.gpsimd.memset(neg_half[:], -0.5)
+
+        h32 = held.tile([P, BLOCKS, N], F32, name="h32")
+        h16 = held.tile([P, BLOCKS, N], BF16, name="h16")
+        q16 = held.tile([P, HEADS, N], BF16, name="q16")
+        k16 = held.tile([P, HEADS, N], BF16, name="k16")
+        o16 = held.tile([P, HEADS, N], BF16, name="o16")
+        v16 = held.tile([P, N // P, D], BF16, name="v16")
+
+        def new_bank(name, dtype=F32, columns=BANK):
+            return banks.tile([P, columns], dtype, tag="bank", name=name)
+
+        ln_ps = new_bank("ln_ps")
+        nc.tensor.matmul(
+            ln_ps[:, 0 : 2 * BLOCKS], ln_rows[:], ident32[0 : 2 * BLOCKS, 0 : 2 * BLOCKS], start=True, stop=True
+        )
+        ln_cols = held.tile([P, 2 * BLOCKS], F32, name="ln_cols")
+        nc.vector.tensor_copy(ln_cols[:], ln_ps[:, 0 : 2 * BLOCKS])
+
+        def look_up(g):
+            for c in range(BLOCKS):
+                for b in (2 * g, 2 * g + 1):
+                    tokens = slice(b * T, (b + 1) * T)
+                    picked = emb_sb[c][:].indirect(offsets[:, b * T // 16 : (b + 1) * T // 16])
+                    nc.vector.tensor_tensor(h32[:, c, tokens], picked, pos_sb[:, c, :], ALU.add)
+                    nc.gpsimd.tensor_copy(h16[:, c, tokens], h32[:, c, tokens])
+
+        def project(w_sb, dst, g):
+            tokens = slice(g * BANK, (g + 1) * BANK)
+            for e in range(BLOCKS):
+                acc = new_bank("acc")
+                for c in range(BLOCKS):
+                    nc.tensor.matmul(
+                        acc[:], w_sb[:, c, e * P : (e + 1) * P], h16[:, c, tokens], start=(c == 0), stop=(c == BLOCKS - 1)
+                    )
+                nc.scalar.copy(dst[:, e, tokens], acc[:])
+
+        def project_values(g):
+            for block in range(g * BANK // P, (g + 1) * BANK // P):
+                acc = new_bank("acc")
+                for c in range(BLOCKS):
+                    nc.tensor.matmul(
+                        acc[:], h16[:, c, block * P : (block + 1) * P], wv_sb[:, c, :], start=(c == 0), stop=(c == BLOCKS - 1)
+                    )
+                nc.scalar.copy(v16[:, block, :], acc[:])
+
+        def softmax_weights(b):
+            t0 = b * T
+            early_ps = new_bank("early_ps")
+            for n in range(HEADS):
+                nc.tensor.matmul(
+                    early_ps[:, n * P : (n + 1) * P], q16[:, n, t0 : t0 + P], k16[:, n, t0 : t0 + P], start=(n == 0), stop=False
+                )
+            nc.tensor.matmul(early_ps[:], ident16[:], mask[:], start=False, stop=True)
+            late_ps = []
+            for pair in range(HEADS // 2):
+                bank = new_bank("late_ps")
+                by_head = bank[:].rearrange("t (i u) -> t i u", i=2)
+                for i in range(2):
+                    n = 2 * pair + i
+                    nc.tensor.matmul(by_head[:, i, :], q16[:, n, t0 + P : t0 + T], k16[:, n, t0 : t0 + T], start=(i == 0), stop=False)
+                nc.tensor.matmul(
+                    by_head[:, :, P:T], ident16[:], mask[:, 0 : 2 * P].rearrange("t (i u) -> t i u", i=2), start=False, stop=True
+                )
+                late_ps.append(by_head)
+
+            top = soft.tile([P, 2 * HEADS], F32, name="top")
+            nc.vector.reduce_max(top[:, 0:HEADS], early_ps[:].rearrange("t (n u) -> t n u", n=HEADS), axis=AXIS.X)
+            for pair in range(HEADS // 2):
+                nc.vector.reduce_max(top[:, HEADS + 2 * pair : HEADS + 2 * pair + 2], late_ps[pair], axis=AXIS.X)
+            shift = soft.tile([P, 2 * HEADS], F32, name="shift")
+            nc.vector.tensor_scalar_mul(shift[:], top[:], -SCALE)
+
+            total = soft.tile([P, 2 * HEADS], F32, name="total")
+            early_exp = soft.tile([P, HEADS, P], F32, name="early_exp")
+            late_exp = soft.tile([P, HEADS, T], F32, name="late_exp")
+            for n in range(HEADS):
+                nc.scalar.activation(
+                    early_exp[:, n, :], early_ps[:, n * P : (n + 1) * P], ACT.Exp,
+                    bias=shift[:, n : n + 1], scale=SCALE, accum_out=total[:, n : n + 1],
+                )
+            for n in range(HEADS):
+                nc.scalar.activation(
+                    late_exp[:, n, :], late_ps[n // 2][:, n % 2, :], ACT.Exp,
+                    bias=shift[:, HEADS + n : HEADS + n + 1], scale=SCALE, accum_out=total[:, HEADS + n : HEADS + n + 1],
+                )
+            inverse = soft.tile([P, 2 * HEADS], F32, name="inverse")
+            nc.vector.reciprocal(inverse[:], total[:])
+            early = soft.tile([P, HEADS, P], BF16, name="early")
+            late = soft.tile([P, HEADS, T], BF16, name="late")
+            for n in range(HEADS):
+                nc.gpsimd.tensor_scalar(early[:, n, :], early_exp[:, n, :], inverse[:, n : n + 1], 1.0, ALU.mult, ALU.mult)
+            for n in range(HEADS):
+                nc.gpsimd.tensor_scalar(
+                    late[:, n, :], late_exp[:, n, :], inverse[:, HEADS + n : HEADS + n + 1], 1.0, ALU.mult, ALU.mult
+                )
+            return early, late
+
+        def flip_weights(early, late):
+            flipped = []
+            for pair in range(HEADS // 2):
+                flip_ps = new_bank("flip_ps", BF16, 2 * 3 * P)
+                for i in range(2):
+                    n = 2 * pair + i
+                    at = i * 3 * P
+                    nc.tensor.transpose(flip_ps[:, at : at + P], early[:, n, :], ident16[:])
+                    nc.tensor.transpose(flip_ps[:, at + P : at + 2 * P], late[:, n, 0:P], ident16[:])
+                    nc.tensor.transpose(flip_ps[:, at + 2 * P : at + 3 * P], late[:, n, P:T], ident16[:])
+                keys_first = soft.tile([P, 2 * 3 * P], BF16, name="keys_first")
+                nc.vector.tensor_copy(keys_first[:], flip_ps[:])
+                flipped.append(keys_first)
+            return flipped
+
+        def mix_values(b, flipped):
+            for pair in range(HEADS // 2):
+                o_ps = new_bank("o_ps")
+                for i in range(2):
+                    n = 2 * pair + i
+                    at = i * 3 * P
+                    head = slice(n * P, (n + 1) * P)
+                    nc.tensor.matmul(
+                        o_ps[:, i * T : (i + 1) * T], v16[:, 2 * b, head], flipped[pair][:, at : at + T], start=True, stop=False
+                    )
+                    nc.tensor.matmul(
+                        o_ps[:, i * T + P : (i + 1) * T], v16[:, 2 * b + 1, head], flipped[pair][:, at + T : at + 3 * P],
+                        start=False, stop=True,
+                    )
+                nc.vector.tensor_copy(
+                    o16[:, 2 * pair : 2 * pair + 2, b * T : (b + 1) * T], o_ps[:].rearrange("d (i t) -> d i t", i=2)
+                )
+
+        def residual_and_norm(block):
+            tokens = slice(block * P, (block + 1) * P)
+            r_ps = new_bank("r_ps")
+            for c in range(BLOCKS):
+                nc.tensor.matmul(
+                    r_ps[:, c * P : (c + 1) * P], h32[:, c, tokens], ident32[:], is_transpose=True, start=(c == 0), stop=False
+                )
+            for c in range(BLOCKS):
+                nc.tensor.matmul(r_ps[:], o16[:, c, tokens], wp_sb[:, c, :], start=False, stop=(c == BLOCKS - 1))
+            stats = norm.tile([P, 6], F32, name="stats")
+            nc.vector.bn_stats(stats[:], r_ps[:])
+            mean_var = norm.tile([P, 2], F32, name="mean_var")
+            nc.vector.bn_aggr(mean_var[:], stats[:])
+            var_eps = norm.tile([P, 1], F32, name="var_eps")
+            nc.vector.tensor_scalar_add(var_eps[:], mean_var[:, 1:2], EPS)
+            rstd = norm.tile([P, 1], F32, name="rstd")
+            nc.gpsimd.tensor_tensor(rstd[:], var_eps[:], neg_half[:], ALU.pow)
+            normed = norm.tile([P, D], F32, name="normed")
+            nc.vector.tensor_scalar(normed[:], r_ps[:], mean_var[:, 0:1], rstd[:], ALU.subtract, ALU.mult)
+            return normed
+
+        def finish(b, normed):
+            for pair in range(BLOCKS // 2):
+                back_ps = new_bank("back_ps")
+                for i in range(2):
+                    e = 2 * pair + i
+                    for half in range(2):
+                        at = i * T + half * P
+                        nc.tensor.transpose(back_ps[:, at : at + P], normed[half][:, e * P : (e + 1) * P], ident32[:])
+                    y = norm.tile([P, T], F32, name="y")
+                    nc.scalar.activation(
+                        y[:], back_ps[:, i * T : (i + 1) * T], ACT.Identity,
+                        bias=ln_cols[:, BLOCKS + e : BLOCKS + e + 1], scale=ln_cols[:, e : e + 1],
+                    )
+                    nc.sync.dma_start(out[e * P : (e + 1) * P, b * T : (b + 1) * T], y[:])
+
+        for g in range(CHUNKS):
+            look_up(g)
+        project(wq_sb, q16, 0)
+        project(wk_sb, k16, 0)
+        project_values(0)
+        normed = {}
+        for g in range(CHUNKS):
+            pair_of_seqs = (2 * g, 2 * g + 1)
+            weights = [softmax_weights(b) for b in pair_of_seqs]
+            if g + 1 < CHUNKS:
+                project(wq_sb, q16, g + 1)
+                project(wk_sb, k16, g + 1)
+            flipped = [flip_weights(early, late) for early, late in weights]
+            if g + 1 < CHUNKS:
+                project_values(g + 1)
+            for b, keys_first in zip(pair_of_seqs, flipped):
+                mix_values(b, keys_first)
+            if g > 0:
+                for b in (2 * g - 2, 2 * g - 1):
+                    finish(b, normed[b])
+            for b in pair_of_seqs:
+                normed[b] = [residual_and_norm(2 * b), residual_and_norm(2 * b + 1)]
+        for b in (SEQS - 2, SEQS - 1):
+            finish(b, normed[b])

@@ -16,7 +16,6 @@ VOCAB, D, T, SEQS, HEADS = 1024, 512, 256, 8, 4
 N = SEQS * T
 BLOCKS = D // P
 BANK = 512
-CHUNKS = N // BANK
 SCALE = 1.0 / math.sqrt(P)
 EPS = 1e-5
 MASKED = -1e30
@@ -28,8 +27,8 @@ def tile_first_decoder_b_kernel(tc, emb, pos, wq, wk, wv, wp, ln_w, ln_b, offs, 
     nc = tc.nc
     with (
         tc.tile_pool(name="held", bufs=1) as held,
-        tc.tile_pool(name="soft", bufs=4) as soft,
-        tc.tile_pool(name="norm", bufs=8) as norm,
+        tc.tile_pool(name="soft", bufs=6) as soft,
+        tc.tile_pool(name="norm", bufs=6) as norm,
         tc.psum_pool(name="banks", bufs=8) as banks,
     ):
         offsets = held.tile([P, N // 16], U16, name="offsets")
@@ -73,33 +72,36 @@ def tile_first_decoder_b_kernel(tc, emb, pos, wq, wk, wv, wp, ln_w, ln_b, offs, 
         def new_bank(name, dtype=F32, columns=BANK):
             return banks.tile([P, columns], dtype, tag="bank", name=name)
 
-        ln_ps = new_bank("ln_ps")
-        nc.tensor.matmul(
-            ln_ps[:, 0 : 2 * BLOCKS], ln_rows[:], ident32[0 : 2 * BLOCKS, 0 : 2 * BLOCKS], start=True, stop=True
-        )
         ln_cols = held.tile([P, 2 * BLOCKS], F32, name="ln_cols")
-        nc.vector.tensor_copy(ln_cols[:], ln_ps[:, 0 : 2 * BLOCKS])
 
-        def look_up(g):
+        def flip_ln():
+            ln_ps = new_bank("ln_ps")
+            nc.tensor.matmul(
+                ln_ps[:, 0 : 2 * BLOCKS], ln_rows[:], ident32[0 : 2 * BLOCKS, 0 : 2 * BLOCKS], start=True, stop=True
+            )
+            nc.vector.tensor_copy(ln_cols[:], ln_ps[:, 0 : 2 * BLOCKS])
+
+        def look_up(b):
+            tokens = slice(b * T, (b + 1) * T)
             for c in range(BLOCKS):
-                for b in (2 * g, 2 * g + 1):
-                    tokens = slice(b * T, (b + 1) * T)
-                    picked = emb_sb[c][:].indirect(offsets[:, b * T // 16 : (b + 1) * T // 16])
-                    nc.vector.tensor_tensor(h32[:, c, tokens], picked, pos_sb[:, c, :], ALU.add)
-                    nc.gpsimd.tensor_copy(h16[:, c, tokens], h32[:, c, tokens])
+                picked = emb_sb[c][:].indirect(offsets[:, b * T // 16 : (b + 1) * T // 16])
+                nc.vector.tensor_tensor(h32[:, c, tokens], picked, pos_sb[:, c, :], ALU.add)
+                nc.gpsimd.tensor_copy(h16[:, c, tokens], h32[:, c, tokens])
 
-        def project(w_sb, dst, g):
-            tokens = slice(g * BANK, (g + 1) * BANK)
-            for e in range(BLOCKS):
-                acc = new_bank("acc")
-                for c in range(BLOCKS):
-                    nc.tensor.matmul(
-                        acc[:], w_sb[:, c, e * P : (e + 1) * P], h16[:, c, tokens], start=(c == 0), stop=(c == BLOCKS - 1)
-                    )
-                nc.scalar.copy(dst[:, e, tokens], acc[:])
+        def project(w_sb, dst, b):
+            tokens = slice(b * T, (b + 1) * T)
+            for pair in range(BLOCKS // 2):
+                acc = new_bank("acc")[:].rearrange("e (i t) -> e i t", i=2)
+                for i in range(2):
+                    e = 2 * pair + i
+                    for c in range(BLOCKS):
+                        nc.tensor.matmul(
+                            acc[:, i, :], w_sb[:, c, e * P : (e + 1) * P], h16[:, c, tokens], start=(c == 0), stop=(c == BLOCKS - 1)
+                        )
+                nc.scalar.copy(dst[:, 2 * pair : 2 * pair + 2, tokens], acc)
 
-        def project_values(g):
-            for block in range(g * BANK // P, (g + 1) * BANK // P):
+        def project_values(b):
+            for block in (2 * b, 2 * b + 1):
                 acc = new_bank("acc")
                 for c in range(BLOCKS):
                     nc.tensor.matmul(
@@ -107,7 +109,7 @@ def tile_first_decoder_b_kernel(tc, emb, pos, wq, wk, wv, wp, ln_w, ln_b, offs, 
                     )
                 nc.scalar.copy(v16[:, block, :], acc[:])
 
-        def softmax_weights(b):
+        def masked_scores(b):
             t0 = b * T
             early_ps = new_bank("early_ps")
             for n in range(HEADS):
@@ -115,60 +117,51 @@ def tile_first_decoder_b_kernel(tc, emb, pos, wq, wk, wv, wp, ln_w, ln_b, offs, 
                     early_ps[:, n * P : (n + 1) * P], q16[:, n, t0 : t0 + P], k16[:, n, t0 : t0 + P], start=(n == 0), stop=False
                 )
             nc.tensor.matmul(early_ps[:], ident16[:], mask[:], start=False, stop=True)
-            late_ps = []
+            scores = [early_ps[:].rearrange("t (n u) -> t n u", n=HEADS)]
             for pair in range(HEADS // 2):
-                bank = new_bank("late_ps")
-                by_head = bank[:].rearrange("t (i u) -> t i u", i=2)
+                late_ps = new_bank("late_ps")[:].rearrange("t (i u) -> t i u", i=2)
                 for i in range(2):
                     n = 2 * pair + i
-                    nc.tensor.matmul(by_head[:, i, :], q16[:, n, t0 + P : t0 + T], k16[:, n, t0 : t0 + T], start=(i == 0), stop=False)
+                    nc.tensor.matmul(late_ps[:, i, :], q16[:, n, t0 + P : t0 + T], k16[:, n, t0 : t0 + T], start=(i == 0), stop=False)
                 nc.tensor.matmul(
-                    by_head[:, :, P:T], ident16[:], mask[:, 0 : 2 * P].rearrange("t (i u) -> t i u", i=2), start=False, stop=True
+                    late_ps[:, :, P:T], ident16[:], mask[:, 0 : 2 * P].rearrange("t (i u) -> t i u", i=2), start=False, stop=True
                 )
-                late_ps.append(by_head)
+                scores.append(late_ps)
+            return scores
 
-            top = soft.tile([P, 2 * HEADS], F32, name="top")
-            nc.vector.reduce_max(top[:, 0:HEADS], early_ps[:].rearrange("t (n u) -> t n u", n=HEADS), axis=AXIS.X)
-            for pair in range(HEADS // 2):
-                nc.vector.reduce_max(top[:, HEADS + 2 * pair : HEADS + 2 * pair + 2], late_ps[pair], axis=AXIS.X)
-            shift = soft.tile([P, 2 * HEADS], F32, name="shift")
+        def exponentials(scores_ps):
+            heads, keys = scores_ps.shape[1], scores_ps.shape[2]
+            top = soft.tile([P, heads], F32, name="top", tag="top")
+            nc.vector.reduce_max(top[:], scores_ps, axis=AXIS.X)
+            shift = soft.tile([P, heads], F32, name="shift", tag="shift")
             nc.vector.tensor_scalar_mul(shift[:], top[:], -SCALE)
+            raised = soft.tile([P, heads, keys], F32, name="raised", tag="raised")
+            total = soft.tile([P, heads], F32, name="total", tag="total")
+            for i in range(heads):
+                nc.scalar.activation(
+                    raised[:, i, :], scores_ps[:, i, :], ACT.Exp,
+                    bias=shift[:, i : i + 1], scale=SCALE, accum_out=total[:, i : i + 1],
+                )
+            return raised, total
 
-            total = soft.tile([P, 2 * HEADS], F32, name="total")
-            early_exp = soft.tile([P, HEADS, P], F32, name="early_exp")
-            late_exp = soft.tile([P, HEADS, T], F32, name="late_exp")
-            for n in range(HEADS):
-                nc.scalar.activation(
-                    early_exp[:, n, :], early_ps[:, n * P : (n + 1) * P], ACT.Exp,
-                    bias=shift[:, n : n + 1], scale=SCALE, accum_out=total[:, n : n + 1],
-                )
-            for n in range(HEADS):
-                nc.scalar.activation(
-                    late_exp[:, n, :], late_ps[n // 2][:, n % 2, :], ACT.Exp,
-                    bias=shift[:, HEADS + n : HEADS + n + 1], scale=SCALE, accum_out=total[:, HEADS + n : HEADS + n + 1],
-                )
-            inverse = soft.tile([P, 2 * HEADS], F32, name="inverse")
+        def normalised(raised, total):
+            heads, keys = raised.shape[1], raised.shape[2]
+            inverse = soft.tile([P, heads], F32, name="inverse", tag="inverse")
             nc.vector.reciprocal(inverse[:], total[:])
-            early = soft.tile([P, HEADS, P], BF16, name="early")
-            late = soft.tile([P, HEADS, T], BF16, name="late")
-            for n in range(HEADS):
-                nc.gpsimd.tensor_scalar(early[:, n, :], early_exp[:, n, :], inverse[:, n : n + 1], 1.0, ALU.mult, ALU.mult)
-            for n in range(HEADS):
-                nc.gpsimd.tensor_scalar(
-                    late[:, n, :], late_exp[:, n, :], inverse[:, HEADS + n : HEADS + n + 1], 1.0, ALU.mult, ALU.mult
-                )
-            return early, late
+            weights = soft.tile([P, heads, keys], BF16, name="weights", tag="weights")
+            for i in range(heads):
+                nc.vector.tensor_scalar_mul(weights[:, i, :], raised[:, i, :], inverse[:, i : i + 1])
+            return weights
 
         def flip_weights(early, late):
             flipped = []
             for pair in range(HEADS // 2):
                 flip_ps = new_bank("flip_ps", BF16, 2 * 3 * P)
                 for i in range(2):
-                    n = 2 * pair + i
                     at = i * 3 * P
-                    nc.tensor.transpose(flip_ps[:, at : at + P], early[:, n, :], ident16[:])
-                    nc.tensor.transpose(flip_ps[:, at + P : at + 2 * P], late[:, n, 0:P], ident16[:])
-                    nc.tensor.transpose(flip_ps[:, at + 2 * P : at + 3 * P], late[:, n, P:T], ident16[:])
+                    nc.tensor.transpose(flip_ps[:, at : at + P], early[:, 2 * pair + i, :], ident16[:])
+                    nc.tensor.transpose(flip_ps[:, at + P : at + 2 * P], late[pair][:, i, 0:P], ident16[:])
+                    nc.tensor.transpose(flip_ps[:, at + 2 * P : at + 3 * P], late[pair][:, i, P:T], ident16[:])
                 keys_first = soft.tile([P, 2 * 3 * P], BF16, name="keys_first")
                 nc.vector.tensor_copy(keys_first[:], flip_ps[:])
                 flipped.append(keys_first)
@@ -178,9 +171,8 @@ def tile_first_decoder_b_kernel(tc, emb, pos, wq, wk, wv, wp, ln_w, ln_b, offs, 
             for pair in range(HEADS // 2):
                 o_ps = new_bank("o_ps")
                 for i in range(2):
-                    n = 2 * pair + i
                     at = i * 3 * P
-                    head = slice(n * P, (n + 1) * P)
+                    head = slice((2 * pair + i) * P, (2 * pair + i + 1) * P)
                     nc.tensor.matmul(
                         o_ps[:, i * T : (i + 1) * T], v16[:, 2 * b, head], flipped[pair][:, at : at + T], start=True, stop=False
                     )
@@ -188,29 +180,36 @@ def tile_first_decoder_b_kernel(tc, emb, pos, wq, wk, wv, wp, ln_w, ln_b, offs, 
                         o_ps[:, i * T + P : (i + 1) * T], v16[:, 2 * b + 1, head], flipped[pair][:, at + T : at + 3 * P],
                         start=False, stop=True,
                     )
-                nc.vector.tensor_copy(
-                    o16[:, 2 * pair : 2 * pair + 2, b * T : (b + 1) * T], o_ps[:].rearrange("d (i t) -> d i t", i=2)
-                )
+                nc.scalar.copy(o16[:, 2 * pair : 2 * pair + 2, b * T : (b + 1) * T], o_ps[:].rearrange("d (i t) -> d i t", i=2))
 
-        def residual_and_norm(block):
-            tokens = slice(block * P, (block + 1) * P)
-            r_ps = new_bank("r_ps")
-            for c in range(BLOCKS):
-                nc.tensor.matmul(
-                    r_ps[:, c * P : (c + 1) * P], h32[:, c, tokens], ident32[:], is_transpose=True, start=(c == 0), stop=False
-                )
-            for c in range(BLOCKS):
-                nc.tensor.matmul(r_ps[:], o16[:, c, tokens], wp_sb[:, c, :], start=False, stop=(c == BLOCKS - 1))
-            stats = norm.tile([P, 6], F32, name="stats")
-            nc.vector.bn_stats(stats[:], r_ps[:])
-            mean_var = norm.tile([P, 2], F32, name="mean_var")
-            nc.vector.bn_aggr(mean_var[:], stats[:])
-            var_eps = norm.tile([P, 1], F32, name="var_eps")
-            nc.vector.tensor_scalar_add(var_eps[:], mean_var[:, 1:2], EPS)
-            rstd = norm.tile([P, 1], F32, name="rstd")
-            nc.gpsimd.tensor_tensor(rstd[:], var_eps[:], neg_half[:], ALU.pow)
-            normed = norm.tile([P, D], F32, name="normed")
-            nc.vector.tensor_scalar(normed[:], r_ps[:], mean_var[:, 0:1], rstd[:], ALU.subtract, ALU.mult)
+        def residual_stats(b):
+            blocks = []
+            for block in (2 * b, 2 * b + 1):
+                tokens = slice(block * P, (block + 1) * P)
+                r_ps = new_bank("r_ps")
+                for c in range(BLOCKS):
+                    nc.tensor.matmul(r_ps[:], o16[:, c, tokens], wp_sb[:, c, :], start=(c == 0), stop=False)
+                for c in range(BLOCKS):
+                    nc.tensor.matmul(
+                        r_ps[:, c * P : (c + 1) * P], h32[:, c, tokens], ident32[:], is_transpose=True, start=False, stop=(c == BLOCKS - 1)
+                    )
+                stats = norm.tile([P, 6], F32, name="stats")
+                nc.vector.bn_stats(stats[:], r_ps[:])
+                mean_var = norm.tile([P, 2], F32, name="mean_var")
+                nc.vector.bn_aggr(mean_var[:], stats[:])
+                var_eps = norm.tile([P, 1], F32, name="var_eps")
+                nc.vector.tensor_scalar_add(var_eps[:], mean_var[:, 1:2], EPS)
+                rstd = norm.tile([P, 1], F32, name="rstd")
+                nc.gpsimd.tensor_tensor(rstd[:], var_eps[:], neg_half[:], ALU.pow)
+                blocks.append((r_ps, mean_var, rstd))
+            return blocks
+
+        def centre(blocks):
+            normed = []
+            for r_ps, mean_var, rstd in blocks:
+                centred = norm.tile([P, D], F32, name="centred")
+                nc.vector.tensor_scalar(centred[:], r_ps[:], mean_var[:, 0:1], rstd[:], ALU.subtract, ALU.mult)
+                normed.append(centred)
             return normed
 
         def finish(b, normed):
@@ -228,27 +227,30 @@ def tile_first_decoder_b_kernel(tc, emb, pos, wq, wk, wv, wp, ln_w, ln_b, offs, 
                     )
                     nc.sync.dma_start(out[e * P : (e + 1) * P, b * T : (b + 1) * T], y[:])
 
-        for g in range(CHUNKS):
-            look_up(g)
+        look_up(0)
+        look_up(1)
         project(wq_sb, q16, 0)
         project(wk_sb, k16, 0)
         project_values(0)
+        flip_ln()
         normed = {}
-        for g in range(CHUNKS):
-            pair_of_seqs = (2 * g, 2 * g + 1)
-            weights = [softmax_weights(b) for b in pair_of_seqs]
-            if g + 1 < CHUNKS:
-                project(wq_sb, q16, g + 1)
-                project(wk_sb, k16, g + 1)
-            flipped = [flip_weights(early, late) for early, late in weights]
-            if g + 1 < CHUNKS:
-                project_values(g + 1)
-            for b, keys_first in zip(pair_of_seqs, flipped):
-                mix_values(b, keys_first)
-            if g > 0:
-                for b in (2 * g - 2, 2 * g - 1):
-                    finish(b, normed[b])
-            for b in pair_of_seqs:
-                normed[b] = [residual_and_norm(2 * b), residual_and_norm(2 * b + 1)]
-        for b in (SEQS - 2, SEQS - 1):
-            finish(b, normed[b])
+        for b in range(SEQS):
+            raised = [exponentials(scores_ps) for scores_ps in masked_scores(b)]
+            if b >= 2:
+                finish(b - 2, normed[b - 2])
+            if b + 2 < SEQS:
+                look_up(b + 2)
+            early, *late = [normalised(powers, total) for powers, total in raised]
+            if b + 1 < SEQS:
+                project(wq_sb, q16, b + 1)
+                project(wk_sb, k16, b + 1)
+            if b >= 1:
+                blocks = residual_stats(b - 1)
+            flipped = flip_weights(early, late)
+            if b >= 1:
+                normed[b - 1] = centre(blocks)
+            if b + 1 < SEQS:
+                project_values(b + 1)
+            mix_values(b, flipped)
+        finish(SEQS - 2, normed[SEQS - 2])
+        finish(SEQS - 1, centre(residual_stats(SEQS - 1)))

@@ -216,10 +216,11 @@ def tile_first_decoder_b_kernel(tc, emb, pos, wq, wk, wv, wp, ln_w, ln_b, offs, 
             for pair in range(BLOCKS // 2):
                 back_ps = new_bank("back_ps")
                 for i in range(2):
-                    e = 2 * pair + i
                     for half in range(2):
-                        at = i * T + half * P
+                        e, at = 2 * pair + i, i * T + half * P
                         nc.tensor.transpose(back_ps[:, at : at + P], normed[half][:, e * P : (e + 1) * P], ident32[:])
+                for i in range(2):
+                    e = 2 * pair + i
                     y = norm.tile([P, T], F32, name="y")
                     nc.scalar.activation(
                         y[:], back_ps[:, i * T : (i + 1) * T], ACT.Identity,

@@ -55,10 +55,14 @@ def tile_first_decoder_b_kernel(tc, emb, pos, wq, wk, wv, wp, ln_w, ln_b, offs, 
         make_identity(nc, ident16[:])
         ident32 = held.tile([P, P], F32, name="ident32")
         make_identity(nc, ident32[:])
-        ahead = held.tile([P, HEADS * P], I32, name="ahead")
-        nc.gpsimd.iota(ahead[:], pattern=[[0, HEADS], [1, P]], base=0, channel_multiplier=-1)
-        mask = held.tile([P, HEADS * P], BF16, name="mask")
-        nc.vector.tensor_scalar(mask[:], ahead[:], 0.0, MASKED, ALU.is_gt, ALU.mult)
+        causal = {}
+        for heads, keys in ((HEADS, P), (2, T)):
+            ahead = held.tile([P, heads * keys], I32, name=f"ahead{keys}")
+            nc.gpsimd.iota(ahead[:], pattern=[[0, heads], [1, keys]], base=P - keys, channel_multiplier=-1)
+            causal[keys] = held.tile([P, heads, keys], F32, name=f"mask{keys}")
+            nc.vector.tensor_scalar(
+                causal[keys][:], ahead[:].rearrange("t (n u) -> t n u", n=heads), 0.0, MASKED, ALU.is_gt, ALU.mult
+            )
         neg_half = held.tile([P, 1], F32, name="neg_half")
         nc.gpsimd.memset(neg_half[:], -0.5)
 
@@ -109,37 +113,33 @@ def tile_first_decoder_b_kernel(tc, emb, pos, wq, wk, wv, wp, ln_w, ln_b, offs, 
                     )
                 nc.scalar.copy(v16[:, block, :], acc[:])
 
-        def masked_scores(b):
+        def scores(b):
             t0 = b * T
-            early_ps = new_bank("early_ps")
+            early_ps = new_bank("early_ps")[:].rearrange("t (n u) -> t n u", n=HEADS)
             for n in range(HEADS):
-                nc.tensor.matmul(
-                    early_ps[:, n * P : (n + 1) * P], q16[:, n, t0 : t0 + P], k16[:, n, t0 : t0 + P], start=(n == 0), stop=False
-                )
-            nc.tensor.matmul(early_ps[:], ident16[:], mask[:], start=False, stop=True)
-            scores = [early_ps[:].rearrange("t (n u) -> t n u", n=HEADS)]
+                nc.tensor.matmul(early_ps[:, n, :], q16[:, n, t0 : t0 + P], k16[:, n, t0 : t0 + P], start=True, stop=True)
+            in_banks = [early_ps]
             for pair in range(HEADS // 2):
                 late_ps = new_bank("late_ps")[:].rearrange("t (i u) -> t i u", i=2)
                 for i in range(2):
                     n = 2 * pair + i
-                    nc.tensor.matmul(late_ps[:, i, :], q16[:, n, t0 + P : t0 + T], k16[:, n, t0 : t0 + T], start=(i == 0), stop=False)
-                nc.tensor.matmul(
-                    late_ps[:, :, P:T], ident16[:], mask[:, 0 : 2 * P].rearrange("t (i u) -> t i u", i=2), start=False, stop=True
-                )
-                scores.append(late_ps)
-            return scores
+                    nc.tensor.matmul(late_ps[:, i, :], q16[:, n, t0 + P : t0 + T], k16[:, n, t0 : t0 + T], start=True, stop=True)
+                in_banks.append(late_ps)
+            return in_banks
 
         def exponentials(scores_ps):
             heads, keys = scores_ps.shape[1], scores_ps.shape[2]
+            masked = soft.tile([P, heads, keys], F32, name="masked", tag="masked")
+            nc.vector.tensor_tensor(masked[:], scores_ps, causal[keys][:], ALU.add)
             top = soft.tile([P, heads], F32, name="top", tag="top")
-            nc.vector.reduce_max(top[:], scores_ps, axis=AXIS.X)
+            nc.vector.reduce_max(top[:], masked[:], axis=AXIS.X)
             shift = soft.tile([P, heads], F32, name="shift", tag="shift")
             nc.vector.tensor_scalar_mul(shift[:], top[:], -SCALE)
             raised = soft.tile([P, heads, keys], F32, name="raised", tag="raised")
             total = soft.tile([P, heads], F32, name="total", tag="total")
             for i in range(heads):
                 nc.scalar.activation(
-                    raised[:, i, :], scores_ps[:, i, :], ACT.Exp,
+                    raised[:, i, :], masked[:, i, :], ACT.Exp,
                     bias=shift[:, i : i + 1], scale=SCALE, accum_out=total[:, i : i + 1],
                 )
             return raised, total
@@ -236,7 +236,7 @@ def tile_first_decoder_b_kernel(tc, emb, pos, wq, wk, wv, wp, ln_w, ln_b, offs, 
         flip_ln()
         normed = {}
         for b in range(SEQS):
-            raised = [exponentials(scores_ps) for scores_ps in masked_scores(b)]
+            raised = [exponentials(scores_ps) for scores_ps in scores(b)]
             if b >= 2:
                 finish(b - 2, normed[b - 2])
             if b + 2 < SEQS:

@@ -29,7 +29,8 @@ def tile_first_decoder_b_kernel(tc, emb, pos, wq, wk, wv, wp, ln_w, ln_b, offs, 
         tc.tile_pool(name="held", bufs=1) as held,
         tc.tile_pool(name="soft", bufs=6) as soft,
         tc.tile_pool(name="norm", bufs=6) as norm,
-        tc.psum_pool(name="banks", bufs=8) as banks,
+        tc.psum_pool(name="banks", bufs=6) as banks,
+        tc.psum_pool(name="sums", bufs=2) as sums,
     ):
         offsets = held.tile([P, N // 16], U16, name="offsets")
         nc.sync.dma_start(offsets[:], offs)
@@ -186,7 +187,7 @@ def tile_first_decoder_b_kernel(tc, emb, pos, wq, wk, wv, wp, ln_w, ln_b, offs, 
             blocks = []
             for block in (2 * b, 2 * b + 1):
                 tokens = slice(block * P, (block + 1) * P)
-                r_ps = new_bank("r_ps")
+                r_ps = sums.tile([P, D], F32, name="r_ps")
                 for c in range(BLOCKS):
                     nc.tensor.matmul(r_ps[:], o16[:, c, tokens], wp_sb[:, c, :], start=(c == 0), stop=False)
                 for c in range(BLOCKS):

@@ -27,10 +27,10 @@ def tile_first_decoder_b_kernel(tc, emb, pos, wq, wk, wv, wp, ln_w, ln_b, offs, 
     nc = tc.nc
     with (
         tc.tile_pool(name="held", bufs=1) as held,
+        tc.tile_pool(name="rounded", bufs=3) as rounded,
         tc.tile_pool(name="soft", bufs=6) as soft,
         tc.tile_pool(name="norm", bufs=6) as norm,
-        tc.psum_pool(name="banks", bufs=6) as banks,
-        tc.psum_pool(name="sums", bufs=2) as sums,
+        tc.psum_pool(name="banks", bufs=8) as banks,
     ):
         offsets = held.tile([P, N // 16], U16, name="offsets")
         nc.sync.dma_start(offsets[:], offs)
@@ -64,11 +64,11 @@ def tile_first_decoder_b_kernel(tc, emb, pos, wq, wk, wv, wp, ln_w, ln_b, offs, 
             nc.vector.tensor_scalar(
                 causal[keys][:], ahead[:].rearrange("t (n u) -> t n u", n=heads), 0.0, MASKED, ALU.is_gt, ALU.mult
             )
-        neg_half = held.tile([P, 1], F32, name="neg_half")
+        neg_half = held.tile([P, 2], F32, name="neg_half")
         nc.gpsimd.memset(neg_half[:], -0.5)
 
         h32 = held.tile([P, BLOCKS, N], F32, name="h32")
-        h16 = held.tile([P, BLOCKS, N], BF16, name="h16")
+        h16 = {}
         q16 = held.tile([P, HEADS, N], BF16, name="q16")
         k16 = held.tile([P, HEADS, N], BF16, name="k16")
         o16 = held.tile([P, HEADS, N], BF16, name="o16")
@@ -88,10 +88,11 @@ def tile_first_decoder_b_kernel(tc, emb, pos, wq, wk, wv, wp, ln_w, ln_b, offs, 
 
         def look_up(b):
             tokens = slice(b * T, (b + 1) * T)
+            h16[b] = rounded.tile([P, BLOCKS, T], BF16, name="h16")
             for c in range(BLOCKS):
                 picked = emb_sb[c][:].indirect(offsets[:, b * T // 16 : (b + 1) * T // 16])
                 nc.vector.tensor_tensor(h32[:, c, tokens], picked, pos_sb[:, c, :], ALU.add)
-                nc.gpsimd.tensor_copy(h16[:, c, tokens], h32[:, c, tokens])
+                nc.scalar.copy(h16[b][:, c, :], h32[:, c, tokens])
 
         def project(w_sb, dst, b):
             tokens = slice(b * T, (b + 1) * T)
@@ -101,18 +102,18 @@ def tile_first_decoder_b_kernel(tc, emb, pos, wq, wk, wv, wp, ln_w, ln_b, offs, 
                     e = 2 * pair + i
                     for c in range(BLOCKS):
                         nc.tensor.matmul(
-                            acc[:, i, :], w_sb[:, c, e * P : (e + 1) * P], h16[:, c, tokens], start=(c == 0), stop=(c == BLOCKS - 1)
+                            acc[:, i, :], w_sb[:, c, e * P : (e + 1) * P], h16[b][:, c, :], start=(c == 0), stop=(c == BLOCKS - 1)
                         )
                 nc.scalar.copy(dst[:, 2 * pair : 2 * pair + 2, tokens], acc)
 
         def project_values(b):
-            for block in (2 * b, 2 * b + 1):
+            for half in range(2):
                 acc = new_bank("acc")
                 for c in range(BLOCKS):
                     nc.tensor.matmul(
-                        acc[:], h16[:, c, block * P : (block + 1) * P], wv_sb[:, c, :], start=(c == 0), stop=(c == BLOCKS - 1)
+                        acc[:], h16[b][:, c, half * P : (half + 1) * P], wv_sb[:, c, :], start=(c == 0), stop=(c == BLOCKS - 1)
                     )
-                nc.scalar.copy(v16[:, block, :], acc[:])
+                nc.scalar.copy(v16[:, 2 * b + half, :], acc[:])
 
         def scores(b):
             t0 = b * T
@@ -184,10 +185,11 @@ def tile_first_decoder_b_kernel(tc, emb, pos, wq, wk, wv, wp, ln_w, ln_b, offs, 
                 nc.scalar.copy(o16[:, 2 * pair : 2 * pair + 2, b * T : (b + 1) * T], o_ps[:].rearrange("d (i t) -> d i t", i=2))
 
         def residual_stats(b):
-            blocks = []
-            for block in (2 * b, 2 * b + 1):
-                tokens = slice(block * P, (block + 1) * P)
-                r_ps = sums.tile([P, D], F32, name="r_ps")
+            r_banks = []
+            mean_var = norm.tile([P, 2, 2], F32, name="mean_var")
+            for half in range(2):
+                tokens = slice((2 * b + half) * P, (2 * b + half + 1) * P)
+                r_ps = new_bank("r_ps")
                 for c in range(BLOCKS):
                     nc.tensor.matmul(r_ps[:], o16[:, c, tokens], wp_sb[:, c, :], start=(c == 0), stop=False)
                 for c in range(BLOCKS):
@@ -196,20 +198,26 @@ def tile_first_decoder_b_kernel(tc, emb, pos, wq, wk, wv, wp, ln_w, ln_b, offs, 
                     )
                 stats = norm.tile([P, 6], F32, name="stats")
                 nc.vector.bn_stats(stats[:], r_ps[:])
-                mean_var = norm.tile([P, 2], F32, name="mean_var")
-                nc.vector.bn_aggr(mean_var[:], stats[:])
-                var_eps = norm.tile([P, 1], F32, name="var_eps")
-                nc.vector.tensor_scalar_add(var_eps[:], mean_var[:, 1:2], EPS)
-                rstd = norm.tile([P, 1], F32, name="rstd")
-                nc.gpsimd.tensor_tensor(rstd[:], var_eps[:], neg_half[:], ALU.pow)
-                blocks.append((r_ps, mean_var, rstd))
-            return blocks
+                nc.vector.bn_aggr(mean_var[:, half, :], stats[:])
+                r_banks.append(r_ps)
+            var_eps = norm.tile([P, 2], F32, name="var_eps")
+            nc.vector.tensor_scalar_add(var_eps[:], mean_var[:, :, 1], EPS)
+            neg_mean = norm.tile([P, 2], F32, name="neg_mean")
+            nc.vector.tensor_scalar_mul(neg_mean[:], mean_var[:, :, 0], -1.0)
+            rstd = norm.tile([P, 2], F32, name="rstd")
+            nc.gpsimd.tensor_tensor(rstd[:], var_eps[:], neg_half[:], ALU.pow)
+            neg_mean_rstd = norm.tile([P, 2], F32, name="neg_mean_rstd")
+            nc.gpsimd.tensor_tensor(neg_mean_rstd[:], neg_mean[:], rstd[:], ALU.mult)
+            return r_banks, rstd, neg_mean_rstd
 
-        def centre(blocks):
+        def centre(r_banks, rstd, neg_mean_rstd):
             normed = []
-            for r_ps, mean_var, rstd in blocks:
+            for half in range(2):
                 centred = norm.tile([P, D], F32, name="centred")
-                nc.vector.tensor_scalar(centred[:], r_ps[:], mean_var[:, 0:1], rstd[:], ALU.subtract, ALU.mult)
+                nc.scalar.activation(
+                    centred[:], r_banks[half][:], ACT.Identity,
+                    bias=neg_mean_rstd[:, half : half + 1], scale=rstd[:, half : half + 1],
+                )
                 normed.append(centred)
             return normed
 
@@ -229,30 +237,39 @@ def tile_first_decoder_b_kernel(tc, emb, pos, wq, wk, wv, wp, ln_w, ln_b, offs, 
                     )
                     nc.sync.dma_start(out[e * P : (e + 1) * P, b * T : (b + 1) * T], y[:])
 
-        look_up(0)
-        look_up(1)
-        project(wq_sb, q16, 0)
-        project(wk_sb, k16, 0)
-        project_values(0)
-        flip_ln()
-        normed = {}
+        def output_stage(x):
+            if x < SEQS:
+                stats_of[x] = residual_stats(x)
+            if 0 <= x - 1 < SEQS:
+                normed[x - 1] = centre(*stats_of[x - 1])
+            if 0 <= x - 2 < SEQS:
+                finish(x - 2, normed[x - 2])
+
+        LEAD = 2
         for b in range(SEQS):
-            raised = [exponentials(scores_ps) for scores_ps in scores(b)]
-            if b >= 2:
-                finish(b - 2, normed[b - 2])
-            if b + 2 < SEQS:
-                look_up(b + 2)
-            early, *late = [normalised(powers, total) for powers, total in raised]
-            if b + 1 < SEQS:
-                project(wq_sb, q16, b + 1)
-                project(wk_sb, k16, b + 1)
-            if b >= 1:
-                blocks = residual_stats(b - 1)
-            flipped = flip_weights(early, late)
-            if b >= 1:
-                normed[b - 1] = centre(blocks)
-            if b + 1 < SEQS:
-                project_values(b + 1)
-            mix_values(b, flipped)
-        finish(SEQS - 2, normed[SEQS - 2])
-        finish(SEQS - 1, centre(residual_stats(SEQS - 1)))
+            look_up(b)
+        for b in range(LEAD):
+            project(wq_sb, q16, b)
+            project(wk_sb, k16, b)
+            project_values(b)
+        flip_ln()
+        weights_of, stats_of, normed = {}, {}, {}
+        for step in range(SEQS + 3):
+            ahead = step + LEAD
+            if step < SEQS:
+                raised = [exponentials(scores_ps) for scores_ps in scores(step)]
+                weights_of[step] = [normalised(powers, total) for powers, total in raised]
+            if ahead < SEQS:
+                project(wq_sb, q16, ahead)
+                project(wk_sb, k16, ahead)
+            else:
+                output_stage(2 * (ahead - SEQS))
+            if 1 <= step <= SEQS:
+                early, *late = weights_of[step - 1]
+                flipped = flip_weights(early, late)
+            if ahead < SEQS:
+                project_values(ahead)
+            else:
+                output_stage(2 * (ahead - SEQS) + 1)
+            if 1 <= step <= SEQS:
+                mix_values(step - 1, flipped)

@@ -19,6 +19,7 @@ BANK = 512
 SCALE = 1.0 / math.sqrt(P)
 EPS = 1e-5
 MASKED = -1e30
+LEAD = 2
 
 FLOPS = 4 * 2 * D * D * N + 2 * 2 * SEQS * HEADS * P * (T * (T + 1) // 2)
 
@@ -30,24 +31,27 @@ def tile_first_decoder_b_kernel(tc, emb, pos, wq, wk, wv, wp, ln_w, ln_b, offs, 
         tc.tile_pool(name="rounded", bufs=3) as rounded,
         tc.tile_pool(name="soft", bufs=6) as soft,
         tc.tile_pool(name="norm", bufs=6) as norm,
+        tc.tile_pool(name="leaving", bufs=12) as leaving,
         tc.psum_pool(name="banks", bufs=8) as banks,
     ):
         offsets = held.tile([P, N // 16], U16, name="offsets")
-        nc.sync.dma_start(offsets[:], offs)
-        pos_sb = held.tile([P, BLOCKS, T], F32, name="pos_sb")
-        nc.scalar.dma_start(pos_sb[:], pos.rearrange("(c p) t -> p c t", p=P))
+        pos_early = held.tile([P, BLOCKS, T], F32, name="pos_early")
+        pos_late = held.tile([P, BLOCKS, T], F32, name="pos_late")
         emb_sb = [held.tile([P, VOCAB], F32, name=f"emb_sb{c}") for c in range(BLOCKS)]
-        for c in range(BLOCKS):
-            queue = nc.sync if c % 2 == 0 else nc.scalar
-            queue.dma_start(emb_sb[c][:], emb[c * P : (c + 1) * P, :])
         wq_sb = held.tile([P, BLOCKS, D], BF16, name="wq_sb")
         wk_sb = held.tile([P, BLOCKS, D], BF16, name="wk_sb")
         wv_sb = held.tile([P, BLOCKS, D], BF16, name="wv_sb")
         wp_sb = held.tile([P, BLOCKS, D], BF16, name="wp_sb")
-        nc.sync.dma_start(wq_sb[:], wq.rearrange("(c p) e -> p c e", p=P))
-        nc.scalar.dma_start(wk_sb[:], wk.rearrange("(c p) e -> p c e", p=P))
+        nc.sync.dma_start(offsets[:], offs)
+        nc.sync.dma_start(emb_sb[0][:], emb[0:P, :])
+        nc.sync.dma_start(pos_early[:], pos.rearrange("(c p) t -> p c t", p=P))
         nc.sync.dma_start(wv_sb[:], wv.rearrange("(c p) e -> p c e", p=P))
-        nc.scalar.dma_start(wp_sb[:], wp.rearrange("(c p) e -> p c e", p=P))
+        for c in range(1, BLOCKS):
+            nc.sync.dma_start(emb_sb[c][:], emb[c * P : (c + 1) * P, :])
+        nc.sync.dma_start(pos_late[:], pos.rearrange("(c p) t -> p c t", p=P))
+        nc.sync.dma_start(wq_sb[:], wq.rearrange("(c p) e -> p c e", p=P))
+        nc.sync.dma_start(wk_sb[:], wk.rearrange("(c p) e -> p c e", p=P))
+        nc.sync.dma_start(wp_sb[:], wp.rearrange("(c p) e -> p c e", p=P))
         ln_rows = held.tile([2 * BLOCKS, P], F32, name="ln_rows")
         nc.gpsimd.dma_start(ln_rows[0:BLOCKS, :], ln_w.rearrange("(c p) o -> c (p o)", p=P))
         nc.gpsimd.dma_start(ln_rows[BLOCKS : 2 * BLOCKS, :], ln_b.rearrange("(c p) o -> c (p o)", p=P))
@@ -86,13 +90,14 @@ def tile_first_decoder_b_kernel(tc, emb, pos, wq, wk, wv, wp, ln_w, ln_b, offs, 
             )
             nc.vector.tensor_copy(ln_cols[:], ln_ps[:, 0 : 2 * BLOCKS])
 
-        def look_up(b):
+        def look_up(b, c):
             tokens = slice(b * T, (b + 1) * T)
-            h16[b] = rounded.tile([P, BLOCKS, T], BF16, name="h16")
-            for c in range(BLOCKS):
-                picked = emb_sb[c][:].indirect(offsets[:, b * T // 16 : (b + 1) * T // 16])
-                nc.vector.tensor_tensor(h32[:, c, tokens], picked, pos_sb[:, c, :], ALU.add)
-                nc.scalar.copy(h16[b][:, c, :], h32[:, c, tokens])
+            if c == 0:
+                h16[b] = rounded.tile([P, BLOCKS, T], BF16, name="h16")
+            picked = emb_sb[c][:].indirect(offsets[:, b * T // 16 : (b + 1) * T // 16])
+            pos_sb = pos_early if b < LEAD else pos_late
+            nc.vector.tensor_tensor(h32[:, c, tokens], picked, pos_sb[:, c, :], ALU.add)
+            nc.scalar.copy(h16[b][:, c, :], h32[:, c, tokens])
 
         def project(w_sb, dst, b):
             tokens = slice(b * T, (b + 1) * T)
@@ -106,14 +111,17 @@ def tile_first_decoder_b_kernel(tc, emb, pos, wq, wk, wv, wp, ln_w, ln_b, offs, 
                         )
                 nc.scalar.copy(dst[:, 2 * pair : 2 * pair + 2, tokens], acc)
 
-        def project_values(b):
-            for half in range(2):
-                acc = new_bank("acc")
-                for c in range(BLOCKS):
+        def project_values(sequences):
+            token_blocks = [(b, half) for b in sequences for half in range(2)]
+            accs = {block: new_bank("acc") for block in token_blocks}
+            for c in range(BLOCKS):
+                for b, half in token_blocks:
                     nc.tensor.matmul(
-                        acc[:], h16[b][:, c, half * P : (half + 1) * P], wv_sb[:, c, :], start=(c == 0), stop=(c == BLOCKS - 1)
+                        accs[b, half][:], h16[b][:, c, half * P : (half + 1) * P], wv_sb[:, c, :],
+                        start=(c == 0), stop=(c == BLOCKS - 1),
                     )
-                nc.scalar.copy(v16[:, 2 * b + half, :], acc[:])
+            for b, half in token_blocks:
+                nc.scalar.copy(v16[:, 2 * b + half, :], accs[b, half][:])
 
         def scores(b):
             t0 = b * T
@@ -230,11 +238,12 @@ def tile_first_decoder_b_kernel(tc, emb, pos, wq, wk, wv, wp, ln_w, ln_b, offs, 
                         nc.tensor.transpose(back_ps[:, at : at + P], normed[half][:, e * P : (e + 1) * P], ident32[:])
                 for i in range(2):
                     e = 2 * pair + i
-                    y = norm.tile([P, T], F32, name="y")
-                    nc.scalar.activation(
-                        y[:], back_ps[:, i * T : (i + 1) * T], ACT.Identity,
-                        bias=ln_cols[:, BLOCKS + e : BLOCKS + e + 1], scale=ln_cols[:, e : e + 1],
-                    )
+                    y = leaving.tile([P, T], F32, name="y")
+                    gain, bias = ln_cols[:, e : e + 1], ln_cols[:, BLOCKS + e : BLOCKS + e + 1]
+                    if pair == 0:
+                        nc.scalar.activation(y[:], back_ps[:, i * T : (i + 1) * T], ACT.Identity, bias=bias, scale=gain)
+                    else:
+                        nc.vector.tensor_scalar(y[:], back_ps[:, i * T : (i + 1) * T], gain, bias, ALU.mult, ALU.add)
                     nc.sync.dma_start(out[e * P : (e + 1) * P, b * T : (b + 1) * T], y[:])
 
         def output_stage(x):
@@ -245,13 +254,16 @@ def tile_first_decoder_b_kernel(tc, emb, pos, wq, wk, wv, wp, ln_w, ln_b, offs, 
             if 0 <= x - 2 < SEQS:
                 finish(x - 2, normed[x - 2])
 
-        LEAD = 2
-        for b in range(SEQS):
-            look_up(b)
+        for c in range(BLOCKS):
+            for b in range(LEAD):
+                look_up(b, c)
+        for b in range(LEAD, SEQS):
+            for c in range(BLOCKS):
+                look_up(b, c)
+        project_values(range(LEAD))
         for b in range(LEAD):
             project(wq_sb, q16, b)
             project(wk_sb, k16, b)
-            project_values(b)
         flip_ln()
         weights_of, stats_of, normed = {}, {}, {}
         for step in range(SEQS + 3):
@@ -259,17 +271,17 @@ def tile_first_decoder_b_kernel(tc, emb, pos, wq, wk, wv, wp, ln_w, ln_b, offs, 
             if step < SEQS:
                 raised = [exponentials(scores_ps) for scores_ps in scores(step)]
                 weights_of[step] = [normalised(powers, total) for powers, total in raised]
+            if 1 <= step <= SEQS:
+                early, *late = weights_of[step - 1]
+                flipped = flip_weights(early, late)
             if ahead < SEQS:
                 project(wq_sb, q16, ahead)
                 project(wk_sb, k16, ahead)
             else:
                 output_stage(2 * (ahead - SEQS))
             if 1 <= step <= SEQS:
-                early, *late = weights_of[step - 1]
-                flipped = flip_weights(early, late)
+                mix_values(step - 1, flipped)
             if ahead < SEQS:
-                project_values(ahead)
+                project_values([ahead])
             else:
                 output_stage(2 * (ahead - SEQS) + 1)
-            if 1 <= step <= SEQS:
-                mix_values(step - 1, flipped)

@@ -20,6 +20,7 @@ SCALE = 1.0 / math.sqrt(P)
 EPS = 1e-5
 MASKED = -1e30
 LEAD = 2
+BACK = 3
 
 FLOPS = 4 * 2 * D * D * N + 2 * 2 * SEQS * HEADS * P * (T * (T + 1) // 2)
 
@@ -28,10 +29,10 @@ def tile_first_decoder_b_kernel(tc, emb, pos, wq, wk, wv, wp, ln_w, ln_b, offs, 
     nc = tc.nc
     with (
         tc.tile_pool(name="held", bufs=1) as held,
-        tc.tile_pool(name="rounded", bufs=3) as rounded,
+        tc.tile_pool(name="rounded", bufs=4) as rounded,
         tc.tile_pool(name="soft", bufs=6) as soft,
-        tc.tile_pool(name="norm", bufs=6) as norm,
-        tc.tile_pool(name="leaving", bufs=12) as leaving,
+        tc.tile_pool(name="norm", bufs=2 * BACK + 2) as norm,
+        tc.tile_pool(name="leaving", bufs=2 * (BACK + 1)) as leaving,
         tc.psum_pool(name="banks", bufs=8) as banks,
     ):
         offsets = held.tile([P, N // 16], U16, name="offsets")
@@ -95,7 +96,7 @@ def tile_first_decoder_b_kernel(tc, emb, pos, wq, wk, wv, wp, ln_w, ln_b, offs, 
             if c == 0:
                 h16[b] = rounded.tile([P, BLOCKS, T], BF16, name="h16")
             picked = emb_sb[c][:].indirect(offsets[:, b * T // 16 : (b + 1) * T // 16])
-            pos_sb = pos_early if b < LEAD else pos_late
+            pos_sb = pos_early if b <= LEAD else pos_late
             nc.vector.tensor_tensor(h32[:, c, tokens], picked, pos_sb[:, c, :], ALU.add)
             nc.scalar.copy(h16[b][:, c, :], h32[:, c, tokens])
 
@@ -236,52 +237,55 @@ def tile_first_decoder_b_kernel(tc, emb, pos, wq, wk, wv, wp, ln_w, ln_b, offs, 
                     for half in range(2):
                         e, at = 2 * pair + i, i * T + half * P
                         nc.tensor.transpose(back_ps[:, at : at + P], normed[half][:, e * P : (e + 1) * P], ident32[:])
+                y = leaving.tile([P, 2, T], F32, name="y")
                 for i in range(2):
                     e = 2 * pair + i
-                    y = leaving.tile([P, T], F32, name="y")
                     gain, bias = ln_cols[:, e : e + 1], ln_cols[:, BLOCKS + e : BLOCKS + e + 1]
                     if pair == 0:
-                        nc.scalar.activation(y[:], back_ps[:, i * T : (i + 1) * T], ACT.Identity, bias=bias, scale=gain)
+                        nc.scalar.activation(y[:, i, :], back_ps[:, i * T : (i + 1) * T], ACT.Identity, bias=bias, scale=gain)
                     else:
-                        nc.vector.tensor_scalar(y[:], back_ps[:, i * T : (i + 1) * T], gain, bias, ALU.mult, ALU.add)
-                    nc.sync.dma_start(out[e * P : (e + 1) * P, b * T : (b + 1) * T], y[:])
+                        nc.vector.tensor_scalar(y[:, i, :], back_ps[:, i * T : (i + 1) * T], gain, bias, ALU.mult, ALU.add)
+                nc.sync.dma_start(
+                    out.rearrange("(e p) j -> p e j", p=P)[:, 2 * pair : 2 * pair + 2, b * T : (b + 1) * T], y[:]
+                )
 
         def output_stage(x):
             if x < SEQS:
                 stats_of[x] = residual_stats(x)
             if 0 <= x - 1 < SEQS:
                 normed[x - 1] = centre(*stats_of[x - 1])
-            if 0 <= x - 2 < SEQS:
-                finish(x - 2, normed[x - 2])
+            if 0 <= x - BACK < SEQS:
+                finish(x - BACK, normed[x - BACK])
 
         for c in range(BLOCKS):
-            for b in range(LEAD):
+            for b in range(LEAD + 1):
                 look_up(b, c)
-        for b in range(LEAD, SEQS):
+        for b in range(LEAD + 1, SEQS):
             for c in range(BLOCKS):
                 look_up(b, c)
-        project_values(range(LEAD))
+        project_values(range(LEAD + 1))
         for b in range(LEAD):
             project(wq_sb, q16, b)
             project(wk_sb, k16, b)
         flip_ln()
         weights_of, stats_of, normed = {}, {}, {}
-        for step in range(SEQS + 3):
+        for step in range(SEQS + 2 + BACK // 2):
             ahead = step + LEAD
-            if step < SEQS:
-                raised = [exponentials(scores_ps) for scores_ps in scores(step)]
-                weights_of[step] = [normalised(powers, total) for powers, total in raised]
             if 1 <= step <= SEQS:
                 early, *late = weights_of[step - 1]
                 flipped = flip_weights(early, late)
+            if step < SEQS:
+                raised = [exponentials(scores_ps) for scores_ps in scores(step)]
             if ahead < SEQS:
                 project(wq_sb, q16, ahead)
                 project(wk_sb, k16, ahead)
             else:
-                output_stage(2 * (ahead - SEQS))
+                output_stage(2 * (ahead - SEQS) + 1)
             if 1 <= step <= SEQS:
                 mix_values(step - 1, flipped)
-            if ahead < SEQS:
-                project_values([ahead])
+            if ahead + 1 < SEQS:
+                project_values([ahead + 1])
             else:
-                output_stage(2 * (ahead - SEQS) + 1)
+                output_stage(2 * (ahead + 1 - SEQS))
+            if step < SEQS:
+                weights_of[step] = [normalised(powers, total) for powers, total in raised]

@@ -44,11 +44,11 @@ def tile_first_decoder_b_kernel(tc, emb, pos, wq, wk, wv, wp, ln_w, ln_b, offs, 
         wv_sb = held.tile([P, BLOCKS, D], BF16, name="wv_sb")
         wp_sb = held.tile([P, BLOCKS, D], BF16, name="wp_sb")
         nc.sync.dma_start(offsets[:], offs)
-        nc.sync.dma_start(emb_sb[0][:], emb[0:P, :])
-        nc.sync.dma_start(pos_early[:], pos.rearrange("(c p) t -> p c t", p=P))
-        nc.sync.dma_start(wv_sb[:], wv.rearrange("(c p) e -> p c e", p=P))
-        for c in range(1, BLOCKS):
+        for c in range(BLOCKS):
             nc.sync.dma_start(emb_sb[c][:], emb[c * P : (c + 1) * P, :])
+            nc.sync.dma_start(pos_early[:, c, :], pos[c * P : (c + 1) * P, :])
+            if c == 1:
+                nc.sync.dma_start(wv_sb[:], wv.rearrange("(c p) e -> p c e", p=P))
         nc.sync.dma_start(pos_late[:], pos.rearrange("(c p) t -> p c t", p=P))
         nc.sync.dma_start(wq_sb[:], wq.rearrange("(c p) e -> p c e", p=P))
         nc.sync.dma_start(wk_sb[:], wk.rearrange("(c p) e -> p c e", p=P))
@@ -231,12 +231,13 @@ def tile_first_decoder_b_kernel(tc, emb, pos, wq, wk, wv, wp, ln_w, ln_b, offs, 
             return normed
 
         def finish(b, normed):
+            back_banks = [new_bank("back_ps") for pair in range(BLOCKS // 2)]
+            for half in range(2):
+                for e in range(BLOCKS):
+                    at = (e % 2) * T + half * P
+                    nc.tensor.transpose(back_banks[e // 2][:, at : at + P], normed[half][:, e * P : (e + 1) * P], ident32[:])
             for pair in range(BLOCKS // 2):
-                back_ps = new_bank("back_ps")
-                for i in range(2):
-                    for half in range(2):
-                        e, at = 2 * pair + i, i * T + half * P
-                        nc.tensor.transpose(back_ps[:, at : at + P], normed[half][:, e * P : (e + 1) * P], ident32[:])
+                back_ps = back_banks[pair]
                 y = leaving.tile([P, 2, T], F32, name="y")
                 for i in range(2):
                     e = 2 * pair + i

@@ -53,9 +53,10 @@ def tile_first_decoder_b_kernel(tc, emb, pos, wq, wk, wv, wp, ln_w, ln_b, offs, 
         nc.sync.dma_start(wq_sb[:], wq.rearrange("(c p) e -> p c e", p=P))
         nc.sync.dma_start(wk_sb[:], wk.rearrange("(c p) e -> p c e", p=P))
         nc.sync.dma_start(wp_sb[:], wp.rearrange("(c p) e -> p c e", p=P))
-        ln_rows = held.tile([2 * BLOCKS, P], F32, name="ln_rows")
-        nc.gpsimd.dma_start(ln_rows[0:BLOCKS, :], ln_w.rearrange("(c p) o -> c (p o)", p=P))
-        nc.gpsimd.dma_start(ln_rows[BLOCKS : 2 * BLOCKS, :], ln_b.rearrange("(c p) o -> c (p o)", p=P))
+        gains = held.tile([P, BLOCKS], F32, name="gains")
+        biases = held.tile([P, BLOCKS], F32, name="biases")
+        nc.sync.dma_start(gains[:], ln_w.rearrange("(e p) o -> p (e o)", p=P))
+        nc.sync.dma_start(biases[:], ln_b.rearrange("(e p) o -> p (e o)", p=P))
 
         ident16 = held.tile([P, P], BF16, name="ident16")
         make_identity(nc, ident16[:])
@@ -81,15 +82,6 @@ def tile_first_decoder_b_kernel(tc, emb, pos, wq, wk, wv, wp, ln_w, ln_b, offs, 
 
         def new_bank(name, dtype=F32, columns=BANK):
             return banks.tile([P, columns], dtype, tag="bank", name=name)
-
-        ln_cols = held.tile([P, 2 * BLOCKS], F32, name="ln_cols")
-
-        def flip_ln():
-            ln_ps = new_bank("ln_ps")
-            nc.tensor.matmul(
-                ln_ps[:, 0 : 2 * BLOCKS], ln_rows[:], ident32[0 : 2 * BLOCKS, 0 : 2 * BLOCKS], start=True, stop=True
-            )
-            nc.vector.tensor_copy(ln_cols[:], ln_ps[:, 0 : 2 * BLOCKS])
 
         def look_up(b, c):
             tokens = slice(b * T, (b + 1) * T)
@@ -241,7 +233,7 @@ def tile_first_decoder_b_kernel(tc, emb, pos, wq, wk, wv, wp, ln_w, ln_b, offs, 
                 y = leaving.tile([P, 2, T], F32, name="y")
                 for i in range(2):
                     e = 2 * pair + i
-                    gain, bias = ln_cols[:, e : e + 1], ln_cols[:, BLOCKS + e : BLOCKS + e + 1]
+                    gain, bias = gains[:, e : e + 1], biases[:, e : e + 1]
                     if pair == 0:
                         nc.scalar.activation(y[:, i, :], back_ps[:, i * T : (i + 1) * T], ACT.Identity, bias=bias, scale=gain)
                     else:
@@ -268,7 +260,6 @@ def tile_first_decoder_b_kernel(tc, emb, pos, wq, wk, wv, wp, ln_w, ln_b, offs, 
         for b in range(LEAD):
             project(wq_sb, q16, b)
             project(wk_sb, k16, b)
-        flip_ln()
         weights_of, stats_of, normed = {}, {}, {}
         for step in range(SEQS + 2 + BACK // 2):
             ahead = step + LEAD

@@ -58,8 +58,6 @@ def tile_first_decoder_b_kernel(tc, emb, pos, wq, wk, wv, wp, ln_w, ln_b, offs, 
         nc.sync.dma_start(gains[:], ln_w.rearrange("(e p) o -> p (e o)", p=P))
         nc.sync.dma_start(biases[:], ln_b.rearrange("(e p) o -> p (e o)", p=P))
 
-        ident16 = held.tile([P, P], BF16, name="ident16")
-        make_identity(nc, ident16[:])
         ident32 = held.tile([P, P], F32, name="ident32")
         make_identity(nc, ident32[:])
         causal = {}
@@ -151,22 +149,22 @@ def tile_first_decoder_b_kernel(tc, emb, pos, wq, wk, wv, wp, ln_w, ln_b, offs, 
             heads, keys = raised.shape[1], raised.shape[2]
             inverse = soft.tile([P, heads], F32, name="inverse", tag="inverse")
             nc.vector.reciprocal(inverse[:], total[:])
-            weights = soft.tile([P, heads, keys], BF16, name="weights", tag="weights")
+            weights = soft.tile([P, heads // 2, keys, 2], BF16, name="weights", tag="weights")
             for i in range(heads):
-                nc.vector.tensor_scalar_mul(weights[:, i, :], raised[:, i, :], inverse[:, i : i + 1])
+                nc.vector.tensor_scalar_mul(weights[:, i // 2, :, i % 2], raised[:, i, :], inverse[:, i : i + 1])
             return weights
 
         def flip_weights(early, late):
             flipped = []
             for pair in range(HEADS // 2):
-                flip_ps = new_bank("flip_ps", BF16, 2 * 3 * P)
-                for i in range(2):
-                    at = i * 3 * P
-                    nc.tensor.transpose(flip_ps[:, at : at + P], early[:, 2 * pair + i, :], ident16[:])
-                    nc.tensor.transpose(flip_ps[:, at + P : at + 2 * P], late[pair][:, i, 0:P], ident16[:])
-                    nc.tensor.transpose(flip_ps[:, at + 2 * P : at + 3 * P], late[pair][:, i, P:T], ident16[:])
-                keys_first = soft.tile([P, 2 * 3 * P], BF16, name="keys_first")
-                nc.vector.tensor_copy(keys_first[:], flip_ps[:])
+                early_words = early[:, pair, :, :].rearrange("t u i -> t (u i)").bitcast(F32)
+                late_words = late[pair][:, 0, :, :].rearrange("t u i -> t (u i)").bitcast(F32)
+                flip_ps = new_bank("flip_ps", F32, 3 * P)
+                nc.tensor.transpose(flip_ps[:, 0:P], early_words, ident32[:])
+                nc.tensor.transpose(flip_ps[:, P : 2 * P], late_words[:, 0:P], ident32[:])
+                nc.tensor.transpose(flip_ps[:, 2 * P : 3 * P], late_words[:, P:T], ident32[:])
+                keys_first = soft.tile([P, 3 * P, 2], BF16, name="keys_first")
+                nc.vector.tensor_copy(keys_first[:].rearrange("u t i -> u (t i)").bitcast(F32), flip_ps[:])
                 flipped.append(keys_first)
             return flipped
 
@@ -174,13 +172,12 @@ def tile_first_decoder_b_kernel(tc, emb, pos, wq, wk, wv, wp, ln_w, ln_b, offs, 
             for pair in range(HEADS // 2):
                 o_ps = new_bank("o_ps")
                 for i in range(2):
-                    at = i * 3 * P
                     head = slice((2 * pair + i) * P, (2 * pair + i + 1) * P)
                     nc.tensor.matmul(
-                        o_ps[:, i * T : (i + 1) * T], v16[:, 2 * b, head], flipped[pair][:, at : at + T], start=True, stop=False
+                        o_ps[:, i * T : (i + 1) * T], v16[:, 2 * b, head], flipped[pair][:, 0:T, i], start=True, stop=False
                     )
                     nc.tensor.matmul(
-                        o_ps[:, i * T + P : (i + 1) * T], v16[:, 2 * b + 1, head], flipped[pair][:, at + T : at + 3 * P],
+                        o_ps[:, i * T + P : (i + 1) * T], v16[:, 2 * b + 1, head], flipped[pair][:, T : 3 * P, i],
                         start=False, stop=True,
                     )
                 nc.scalar.copy(o16[:, 2 * pair : 2 * pair + 2, b * T : (b + 1) * T], o_ps[:].rearrange("d (i t) -> d i t", i=2))

@@ -47,8 +47,7 @@ def tile_first_decoder_b_kernel(tc, emb, pos, wq, wk, wv, wp, ln_w, ln_b, offs, 
         for c in range(BLOCKS):
             nc.sync.dma_start(emb_sb[c][:], emb[c * P : (c + 1) * P, :])
             nc.sync.dma_start(pos_early[:, c, :], pos[c * P : (c + 1) * P, :])
-            if c == 1:
-                nc.sync.dma_start(wv_sb[:], wv.rearrange("(c p) e -> p c e", p=P))
+            nc.sync.dma_start(wv_sb[:, c, :], wv[c * P : (c + 1) * P, :])
         nc.sync.dma_start(pos_late[:], pos.rearrange("(c p) t -> p c t", p=P))
         nc.sync.dma_start(wq_sb[:], wq.rearrange("(c p) e -> p c e", p=P))
         nc.sync.dma_start(wk_sb[:], wk.rearrange("(c p) e -> p c e", p=P))
@@ -70,6 +69,8 @@ def tile_first_decoder_b_kernel(tc, emb, pos, wq, wk, wv, wp, ln_w, ln_b, offs, 
             )
         neg_half = held.tile([P, 2], F32, name="neg_half")
         nc.gpsimd.memset(neg_half[:], -0.5)
+        eps = held.tile([P, 1], F32, name="eps")
+        nc.gpsimd.memset(eps[:], EPS)
 
         h32 = held.tile([P, BLOCKS, N], F32, name="h32")
         h16 = {}
@@ -182,7 +183,7 @@ def tile_first_decoder_b_kernel(tc, emb, pos, wq, wk, wv, wp, ln_w, ln_b, offs, 
                     )
                 nc.scalar.copy(o16[:, 2 * pair : 2 * pair + 2, b * T : (b + 1) * T], o_ps[:].rearrange("d (i t) -> d i t", i=2))
 
-        def residual_stats(b):
+        def residual_stats(b, softmax_ended):
             r_banks = []
             mean_var = norm.tile([P, 2, 2], F32, name="mean_var")
             for half in range(2):
@@ -198,24 +199,32 @@ def tile_first_decoder_b_kernel(tc, emb, pos, wq, wk, wv, wp, ln_w, ln_b, offs, 
                 nc.vector.bn_stats(stats[:], r_ps[:])
                 nc.vector.bn_aggr(mean_var[:, half, :], stats[:])
                 r_banks.append(r_ps)
-            var_eps = norm.tile([P, 2], F32, name="var_eps")
-            nc.vector.tensor_scalar_add(var_eps[:], mean_var[:, :, 1], EPS)
-            neg_mean = norm.tile([P, 2], F32, name="neg_mean")
-            nc.vector.tensor_scalar_mul(neg_mean[:], mean_var[:, :, 0], -1.0)
+            mean = mean_var[:, :, 0]
             rstd = norm.tile([P, 2], F32, name="rstd")
-            nc.gpsimd.tensor_tensor(rstd[:], var_eps[:], neg_half[:], ALU.pow)
             neg_mean_rstd = norm.tile([P, 2], F32, name="neg_mean_rstd")
-            nc.gpsimd.tensor_tensor(neg_mean_rstd[:], neg_mean[:], rstd[:], ALU.mult)
-            return r_banks, rstd, neg_mean_rstd
+            if softmax_ended:
+                nc.scalar.activation(rstd[:], mean_var[:, :, 1], ACT.Abs_reciprocal_sqrt, bias=eps[:])
+                nc.vector.scalar_tensor_tensor(neg_mean_rstd[:], mean, -1.0, rstd[:], ALU.mult, ALU.mult)
+            else:
+                var_eps = norm.tile([P, 2], F32, name="var_eps")
+                nc.vector.tensor_scalar_add(var_eps[:], mean_var[:, :, 1], EPS)
+                neg_mean = norm.tile([P, 2], F32, name="neg_mean")
+                nc.vector.tensor_scalar_mul(neg_mean[:], mean, -1.0)
+                nc.gpsimd.tensor_tensor(rstd[:], var_eps[:], neg_half[:], ALU.pow)
+                nc.gpsimd.tensor_tensor(neg_mean_rstd[:], neg_mean[:], rstd[:], ALU.mult)
+            return r_banks, mean, rstd, neg_mean_rstd
 
-        def centre(r_banks, rstd, neg_mean_rstd):
+        def centre(softmax_ended, r_banks, mean, rstd, neg_mean_rstd):
             normed = []
             for half in range(2):
                 centred = norm.tile([P, D], F32, name="centred")
-                nc.scalar.activation(
-                    centred[:], r_banks[half][:], ACT.Identity,
-                    bias=neg_mean_rstd[:, half : half + 1], scale=rstd[:, half : half + 1],
-                )
+                column = slice(half, half + 1)
+                if softmax_ended and half == 1:
+                    nc.vector.tensor_scalar(centred[:], r_banks[half][:], mean[:, column], rstd[:, column], ALU.subtract, ALU.mult)
+                else:
+                    nc.scalar.activation(
+                        centred[:], r_banks[half][:], ACT.Identity, bias=neg_mean_rstd[:, column], scale=rstd[:, column]
+                    )
                 normed.append(centred)
             return normed
 
@@ -239,11 +248,11 @@ def tile_first_decoder_b_kernel(tc, emb, pos, wq, wk, wv, wp, ln_w, ln_b, offs, 
                     out.rearrange("(e p) j -> p e j", p=P)[:, 2 * pair : 2 * pair + 2, b * T : (b + 1) * T], y[:]
                 )
 
-        def output_stage(x):
+        def output_stage(x, softmax_ended):
             if x < SEQS:
-                stats_of[x] = residual_stats(x)
+                stats_of[x] = residual_stats(x, softmax_ended)
             if 0 <= x - 1 < SEQS:
-                normed[x - 1] = centre(*stats_of[x - 1])
+                normed[x - 1] = centre(softmax_ended, *stats_of[x - 1])
             if 0 <= x - BACK < SEQS:
                 finish(x - BACK, normed[x - BACK])
 
@@ -269,12 +278,12 @@ def tile_first_decoder_b_kernel(tc, emb, pos, wq, wk, wv, wp, ln_w, ln_b, offs, 
                 project(wq_sb, q16, ahead)
                 project(wk_sb, k16, ahead)
             else:
-                output_stage(2 * (ahead - SEQS) + 1)
+                output_stage(2 * (ahead - SEQS) + 1, step >= SEQS)
             if 1 <= step <= SEQS:
                 mix_values(step - 1, flipped)
             if ahead + 1 < SEQS:
                 project_values([ahead + 1])
             else:
-                output_stage(2 * (ahead + 1 - SEQS))
+                output_stage(2 * (ahead + 1 - SEQS), step >= SEQS)
             if step < SEQS:
                 weights_of[step] = [normalised(powers, total) for powers, total in raised]

@@ -155,7 +155,7 @@ def tile_first_decoder_b_kernel(tc, emb, pos, wq, wk, wv, wp, ln_w, ln_b, offs, 
                 nc.vector.tensor_scalar_mul(weights[:, i // 2, :, i % 2], raised[:, i, :], inverse[:, i : i + 1])
             return weights
 
-        def flip_weights(early, late):
+        def flip_weights(early, *late):
             flipped = []
             for pair in range(HEADS // 2):
                 early_words = early[:, pair, :, :].rearrange("t u i -> t (u i)").bitcast(F32)
@@ -269,9 +269,8 @@ def tile_first_decoder_b_kernel(tc, emb, pos, wq, wk, wv, wp, ln_w, ln_b, offs, 
         weights_of, stats_of, normed = {}, {}, {}
         for step in range(SEQS + 2 + BACK // 2):
             ahead = step + LEAD
-            if 1 <= step <= SEQS:
-                early, *late = weights_of[step - 1]
-                flipped = flip_weights(early, late)
+            if step == SEQS:
+                flipped = flip_weights(*weights_of[step - 1])
             if step < SEQS:
                 raised = [exponentials(scores_ps) for scores_ps in scores(step)]
             if ahead < SEQS:
@@ -279,11 +278,15 @@ def tile_first_decoder_b_kernel(tc, emb, pos, wq, wk, wv, wp, ln_w, ln_b, offs, 
                 project(wk_sb, k16, ahead)
             else:
                 output_stage(2 * (ahead - SEQS) + 1, step >= SEQS)
-            if 1 <= step <= SEQS:
+            if 1 <= step < SEQS:
+                flipped = flip_weights(*weights_of[step - 1])
+            if step == SEQS:
                 mix_values(step - 1, flipped)
             if ahead + 1 < SEQS:
                 project_values([ahead + 1])
             else:
                 output_stage(2 * (ahead + 1 - SEQS), step >= SEQS)
+            if 1 <= step < SEQS:
+                mix_values(step - 1, flipped)
             if step < SEQS:
                 weights_of[step] = [normalised(powers, total) for powers, total in raised]

@@ -269,24 +269,25 @@ def tile_first_decoder_b_kernel(tc, emb, pos, wq, wk, wv, wp, ln_w, ln_b, offs, 
         weights_of, stats_of, normed = {}, {}, {}
         for step in range(SEQS + 2 + BACK // 2):
             ahead = step + LEAD
-            if step == SEQS:
+            projecting = ahead < SEQS
+            if not projecting and step <= SEQS:
                 flipped = flip_weights(*weights_of[step - 1])
             if step < SEQS:
                 raised = [exponentials(scores_ps) for scores_ps in scores(step)]
-            if ahead < SEQS:
+            if projecting:
                 project(wq_sb, q16, ahead)
                 project(wk_sb, k16, ahead)
+                if step >= 1:
+                    flipped = flip_weights(*weights_of[step - 1])
             else:
                 output_stage(2 * (ahead - SEQS) + 1, step >= SEQS)
-            if 1 <= step < SEQS:
-                flipped = flip_weights(*weights_of[step - 1])
-            if step == SEQS:
-                mix_values(step - 1, flipped)
+                if step <= SEQS:
+                    mix_values(step - 1, flipped)
             if ahead + 1 < SEQS:
                 project_values([ahead + 1])
             else:
                 output_stage(2 * (ahead + 1 - SEQS), step >= SEQS)
-            if 1 <= step < SEQS:
+            if projecting and step >= 1:
                 mix_values(step - 1, flipped)
             if step < SEQS:
                 weights_of[step] = [normalised(powers, total) for powers, total in raised]

@@ -29,7 +29,7 @@ def tile_first_decoder_b_kernel(tc, emb, pos, wq, wk, wv, wp, ln_w, ln_b, offs, 
     nc = tc.nc
     with (
         tc.tile_pool(name="held", bufs=1) as held,
-        tc.tile_pool(name="rounded", bufs=4) as rounded,
+        tc.tile_pool(name="rounded", bufs=2) as rounded,
         tc.tile_pool(name="soft", bufs=6) as soft,
         tc.tile_pool(name="norm", bufs=2 * BACK + 2) as norm,
         tc.tile_pool(name="leaving", bufs=2 * (BACK + 1)) as leaving,
@@ -84,24 +84,24 @@ def tile_first_decoder_b_kernel(tc, emb, pos, wq, wk, wv, wp, ln_w, ln_b, offs, 
 
         def look_up(b, c):
             tokens = slice(b * T, (b + 1) * T)
-            if c == 0:
-                h16[b] = rounded.tile([P, BLOCKS, T], BF16, name="h16")
+            pair, place = b // 2, b % 2
+            if pair not in h16:
+                h16[pair] = rounded.tile([P, BLOCKS, 2, T], BF16, name="h16")
             picked = emb_sb[c][:].indirect(offsets[:, b * T // 16 : (b + 1) * T // 16])
             pos_sb = pos_early if b <= LEAD else pos_late
             nc.vector.tensor_tensor(h32[:, c, tokens], picked, pos_sb[:, c, :], ALU.add)
-            nc.scalar.copy(h16[b][:, c, :], h32[:, c, tokens])
+            nc.scalar.copy(h16[pair][:, c, place, :], h32[:, c, tokens])
 
-        def project(w_sb, dst, b):
-            tokens = slice(b * T, (b + 1) * T)
-            for pair in range(BLOCKS // 2):
-                acc = new_bank("acc")[:].rearrange("e (i t) -> e i t", i=2)
-                for i in range(2):
-                    e = 2 * pair + i
+        def project(w_sb, dst, b, count):
+            place = b % 2
+            for e0 in range(0, BLOCKS, 2 // count):
+                acc = new_bank("acc")[:].rearrange("e (i t) -> e i t", t=count * T)
+                for i in range(2 // count):
+                    columns = slice((e0 + i) * P, (e0 + i + 1) * P)
                     for c in range(BLOCKS):
-                        nc.tensor.matmul(
-                            acc[:, i, :], w_sb[:, c, e * P : (e + 1) * P], h16[b][:, c, :], start=(c == 0), stop=(c == BLOCKS - 1)
-                        )
-                nc.scalar.copy(dst[:, 2 * pair : 2 * pair + 2, tokens], acc)
+                        h_block = h16[b // 2][:, c, place : place + count, :].rearrange("p i t -> p (i t)")
+                        nc.tensor.matmul(acc[:, i, :], w_sb[:, c, columns], h_block, start=(c == 0), stop=(c == BLOCKS - 1))
+                nc.scalar.copy(dst[:, e0 : e0 + 2 // count, b * T : (b + count) * T], acc)
 
         def project_values(sequences):
             token_blocks = [(b, half) for b in sequences for half in range(2)]
@@ -109,7 +109,7 @@ def tile_first_decoder_b_kernel(tc, emb, pos, wq, wk, wv, wp, ln_w, ln_b, offs, 
             for c in range(BLOCKS):
                 for b, half in token_blocks:
                     nc.tensor.matmul(
-                        accs[b, half][:], h16[b][:, c, half * P : (half + 1) * P], wv_sb[:, c, :],
+                        accs[b, half][:], h16[b // 2][:, c, b % 2, half * P : (half + 1) * P], wv_sb[:, c, :],
                         start=(c == 0), stop=(c == BLOCKS - 1),
                     )
             for b, half in token_blocks:
@@ -264,8 +264,8 @@ def tile_first_decoder_b_kernel(tc, emb, pos, wq, wk, wv, wp, ln_w, ln_b, offs, 
                 look_up(b, c)
         project_values(range(LEAD + 1))
         for b in range(LEAD):
-            project(wq_sb, q16, b)
-            project(wk_sb, k16, b)
+            project(wq_sb, q16, b, 1)
+            project(wk_sb, k16, b, 1)
         weights_of, stats_of, normed = {}, {}, {}
         for step in range(SEQS + 2 + BACK // 2):
             ahead = step + LEAD
@@ -275,8 +275,10 @@ def tile_first_decoder_b_kernel(tc, emb, pos, wq, wk, wv, wp, ln_w, ln_b, offs, 
             if step < SEQS:
                 raised = [exponentials(scores_ps) for scores_ps in scores(step)]
             if projecting:
-                project(wq_sb, q16, ahead)
-                project(wk_sb, k16, ahead)
+                if step % 2 == 0:
+                    project(wq_sb, q16, ahead, 2)
+                else:
+                    project(wk_sb, k16, ahead - 1, 2)
                 if step >= 1:
                     flipped = flip_weights(*weights_of[step - 1])
             else:

@@ -187,18 +187,21 @@ def tile_first_decoder_b_kernel(tc, emb, pos, wq, wk, wv, wp, ln_w, ln_b, offs, 
             r_banks = []
             mean_var = norm.tile([P, 2, 2], F32, name="mean_var")
             for half in range(2):
-                tokens = slice((2 * b + half) * P, (2 * b + half + 1) * P)
                 r_ps = new_bank("r_ps")
                 for c in range(BLOCKS):
+                    tokens = slice((2 * b + half) * P, (2 * b + half + 1) * P)
                     nc.tensor.matmul(r_ps[:], o16[:, c, tokens], wp_sb[:, c, :], start=(c == 0), stop=False)
+                r_banks.append(r_ps)
+            for half in range(2):
+                r_ps = r_banks[half]
                 for c in range(BLOCKS):
+                    tokens = slice((2 * b + half) * P, (2 * b + half + 1) * P)
                     nc.tensor.matmul(
                         r_ps[:, c * P : (c + 1) * P], h32[:, c, tokens], ident32[:], is_transpose=True, start=False, stop=(c == BLOCKS - 1)
                     )
                 stats = norm.tile([P, 6], F32, name="stats")
                 nc.vector.bn_stats(stats[:], r_ps[:])
                 nc.vector.bn_aggr(mean_var[:, half, :], stats[:])
-                r_banks.append(r_ps)
             mean = mean_var[:, :, 0]
             rstd = norm.tile([P, 2], F32, name="rstd")
             neg_mean_rstd = norm.tile([P, 2], F32, name="neg_mean_rstd")

import math

import concourse.mybir as mybir
from concourse.masks import make_identity

F32 = mybir.dt.float32
BF16 = mybir.dt.bfloat16
U16 = mybir.dt.uint16
I32 = mybir.dt.int32
ALU = mybir.AluOpType
ACT = mybir.ActivationFunctionType
AXIS = mybir.AxisListType

P = 128
VOCAB, D, T, SEQS, HEADS = 1024, 512, 256, 8, 4
N = SEQS * T
BLOCKS = D // P
BANK = 512
SCALE = 1.0 / math.sqrt(P)
EPS = 1e-5
MASKED = -1e30
LEAD = 2
BACK = 3

FLOPS = 4 * 2 * D * D * N + 2 * 2 * SEQS * HEADS * P * (T * (T + 1) // 2)


def tile_first_decoder_b_kernel(tc, emb, pos, wq, wk, wv, wp, ln_w, ln_b, offs, out):
    nc = tc.nc
    with (
        tc.tile_pool(name="held", bufs=1) as held,
        tc.tile_pool(name="rounded", bufs=2) as rounded,
        tc.tile_pool(name="soft", bufs=6) as soft,
        tc.tile_pool(name="norm", bufs=2 * BACK + 2) as norm,
        tc.tile_pool(name="leaving", bufs=2 * (BACK + 1)) as leaving,
        tc.psum_pool(name="banks", bufs=8) as banks,
    ):
        offsets = held.tile([P, N // 16], U16, name="offsets")
        pos_early = held.tile([P, BLOCKS, T], F32, name="pos_early")
        pos_late = held.tile([P, BLOCKS, T], F32, name="pos_late")
        emb_sb = [held.tile([P, VOCAB], F32, name=f"emb_sb{c}") for c in range(BLOCKS)]
        wq_sb = held.tile([P, BLOCKS, D], BF16, name="wq_sb")
        wk_sb = held.tile([P, BLOCKS, D], BF16, name="wk_sb")
        wv_sb = held.tile([P, BLOCKS, D], BF16, name="wv_sb")
        wp_sb = held.tile([P, BLOCKS, D], BF16, name="wp_sb")
        nc.sync.dma_start(offsets[:], offs)
        for c in range(BLOCKS):
            nc.sync.dma_start(emb_sb[c][:], emb[c * P : (c + 1) * P, :])
            nc.sync.dma_start(pos_early[:, c, :], pos[c * P : (c + 1) * P, :])
            nc.sync.dma_start(wv_sb[:, c, :], wv[c * P : (c + 1) * P, :])
        nc.sync.dma_start(pos_late[:], pos.rearrange("(c p) t -> p c t", p=P))
        nc.sync.dma_start(wq_sb[:], wq.rearrange("(c p) e -> p c e", p=P))
        nc.sync.dma_start(wk_sb[:], wk.rearrange("(c p) e -> p c e", p=P))
        nc.sync.dma_start(wp_sb[:], wp.rearrange("(c p) e -> p c e", p=P))
        gains = held.tile([P, BLOCKS], F32, name="gains")
        biases = held.tile([P, BLOCKS], F32, name="biases")
        nc.sync.dma_start(gains[:], ln_w.rearrange("(e p) o -> p (e o)", p=P))
        nc.sync.dma_start(biases[:], ln_b.rearrange("(e p) o -> p (e o)", p=P))

        ident32 = held.tile([P, P], F32, name="ident32")
        make_identity(nc, ident32[:])
        causal = {}
        for heads, keys in ((HEADS, P), (2, T)):
            ahead = held.tile([P, heads * keys], I32, name=f"ahead{keys}")
            nc.gpsimd.iota(ahead[:], pattern=[[0, heads], [1, keys]], base=P - keys, channel_multiplier=-1)
            causal[keys] = held.tile([P, heads, keys], F32, name=f"mask{keys}")
            nc.vector.tensor_scalar(
                causal[keys][:], ahead[:].rearrange("t (n u) -> t n u", n=heads), 0.0, MASKED, ALU.is_gt, ALU.mult
            )
        neg_half = held.tile([P, 2], F32, name="neg_half")
        nc.gpsimd.memset(neg_half[:], -0.5)
        eps = held.tile([P, 1], F32, name="eps")
        nc.gpsimd.memset(eps[:], EPS)

        h32 = held.tile([P, BLOCKS, N], F32, name="h32")
        h16 = {}
        q16 = held.tile([P, HEADS, N], BF16, name="q16")
        k16 = held.tile([P, HEADS, N], BF16, name="k16")
        o16 = held.tile([P, HEADS, N], BF16, name="o16")
        v16 = held.tile([P, N // P, D], BF16, name="v16")

        def new_bank(name, dtype=F32, columns=BANK):
            return banks.tile([P, columns], dtype, tag="bank", name=name)

        def look_up(b, c):
            tokens = slice(b * T, (b + 1) * T)
            pair, place = b // 2, b % 2
            if pair not in h16:
                h16[pair] = rounded.tile([P, BLOCKS, 2, T], BF16, name="h16")
            picked = emb_sb[c][:].indirect(offsets[:, b * T // 16 : (b + 1) * T // 16])
            pos_sb = pos_early if b <= LEAD else pos_late
            nc.vector.tensor_tensor(h32[:, c, tokens], picked, pos_sb[:, c, :], ALU.add)
            nc.scalar.copy(h16[pair][:, c, place, :], h32[:, c, tokens])

        def project(w_sb, dst, b, count):
            place = b % 2
            for e0 in range(0, BLOCKS, 2 // count):
                acc = new_bank("acc")[:].rearrange("e (i t) -> e i t", t=count * T)
                for i in range(2 // count):
                    columns = slice((e0 + i) * P, (e0 + i + 1) * P)
                    for c in range(BLOCKS):
                        h_block = h16[b // 2][:, c, place : place + count, :].rearrange("p i t -> p (i t)")
                        nc.tensor.matmul(acc[:, i, :], w_sb[:, c, columns], h_block, start=(c == 0), stop=(c == BLOCKS - 1))
                nc.scalar.copy(dst[:, e0 : e0 + 2 // count, b * T : (b + count) * T], acc)

        def project_values(sequences):
            token_blocks = [(b, half) for b in sequences for half in range(2)]
            accs = {block: new_bank("acc") for block in token_blocks}
            for c in range(BLOCKS):
                for b, half in token_blocks:
                    nc.tensor.matmul(
                        accs[b, half][:], h16[b // 2][:, c, b % 2, half * P : (half + 1) * P], wv_sb[:, c, :],
                        start=(c == 0), stop=(c == BLOCKS - 1),
                    )
            for b, half in token_blocks:
                nc.scalar.copy(v16[:, 2 * b + half, :], accs[b, half][:])

        def scores(b):
            t0 = b * T
            early_ps = new_bank("early_ps")[:].rearrange("t (n u) -> t n u", n=HEADS)
            for n in range(HEADS):
                nc.tensor.matmul(early_ps[:, n, :], q16[:, n, t0 : t0 + P], k16[:, n, t0 : t0 + P], start=True, stop=True)
            in_banks = [early_ps]
            for pair in range(HEADS // 2):
                late_ps = new_bank("late_ps")[:].rearrange("t (i u) -> t i u", i=2)
                for i in range(2):
                    n = 2 * pair + i
                    nc.tensor.matmul(late_ps[:, i, :], q16[:, n, t0 + P : t0 + T], k16[:, n, t0 : t0 + T], start=True, stop=True)
                in_banks.append(late_ps)
            return in_banks

        def exponentials(scores_ps):
            heads, keys = scores_ps.shape[1], scores_ps.shape[2]
            masked = soft.tile([P, heads, keys], F32, name="masked", tag="masked")
            nc.vector.tensor_tensor(masked[:], scores_ps, causal[keys][:], ALU.add)
            top = soft.tile([P, heads], F32, name="top", tag="top")
            nc.vector.reduce_max(top[:], masked[:], axis=AXIS.X)
            shift = soft.tile([P, heads], F32, name="shift", tag="shift")
            nc.vector.tensor_scalar_mul(shift[:], top[:], -SCALE)
            raised = soft.tile([P, heads, keys], F32, name="raised", tag="raised")
            total = soft.tile([P, heads], F32, name="total", tag="total")
            for i in range(heads):
                nc.scalar.activation(
                    raised[:, i, :], masked[:, i, :], ACT.Exp,
                    bias=shift[:, i : i + 1], scale=SCALE, accum_out=total[:, i : i + 1],
                )
            return raised, total

        def normalised(raised, total):
            heads, keys = raised.shape[1], raised.shape[2]
            inverse = soft.tile([P, heads], F32, name="inverse", tag="inverse")
            nc.vector.reciprocal(inverse[:], total[:])
            weights = soft.tile([P, heads // 2, keys, 2], BF16, name="weights", tag="weights")
            for i in range(heads):
                nc.vector.tensor_scalar_mul(weights[:, i // 2, :, i % 2], raised[:, i, :], inverse[:, i : i + 1])
            return weights

        def flip_weights(early, *late):
            flipped = []
            for pair in range(HEADS // 2):
                early_words = early[:, pair, :, :].rearrange("t u i -> t (u i)").bitcast(F32)
                late_words = late[pair][:, 0, :, :].rearrange("t u i -> t (u i)").bitcast(F32)
                flip_ps = new_bank("flip_ps", F32, 3 * P)
                nc.tensor.transpose(flip_ps[:, 0:P], early_words, ident32[:])
                nc.tensor.transpose(flip_ps[:, P : 2 * P], late_words[:, 0:P], ident32[:])
                nc.tensor.transpose(flip_ps[:, 2 * P : 3 * P], late_words[:, P:T], ident32[:])
                keys_first = soft.tile([P, 3 * P, 2], BF16, name="keys_first")
                nc.vector.tensor_copy(keys_first[:].rearrange("u t i -> u (t i)").bitcast(F32), flip_ps[:])
                flipped.append(keys_first)
            return flipped

        def mix_values(b, flipped):
            for pair in range(HEADS // 2):
                o_ps = new_bank("o_ps")
                for i in range(2):
                    head = slice((2 * pair + i) * P, (2 * pair + i + 1) * P)
                    nc.tensor.matmul(
                        o_ps[:, i * T : (i + 1) * T], v16[:, 2 * b, head], flipped[pair][:, 0:T, i], start=True, stop=False
                    )
                    nc.tensor.matmul(
                        o_ps[:, i * T + P : (i + 1) * T], v16[:, 2 * b + 1, head], flipped[pair][:, T : 3 * P, i],
                        start=False, stop=True,
                    )
                nc.scalar.copy(o16[:, 2 * pair : 2 * pair + 2, b * T : (b + 1) * T], o_ps[:].rearrange("d (i t) -> d i t", i=2))

        def residual_stats(b, softmax_ended):
            r_banks = []
            mean_var = norm.tile([P, 2, 2], F32, name="mean_var")
            for half in range(2):
                r_ps = new_bank("r_ps")
                for c in range(BLOCKS):
                    tokens = slice((2 * b + half) * P, (2 * b + half + 1) * P)
                    nc.tensor.matmul(r_ps[:], o16[:, c, tokens], wp_sb[:, c, :], start=(c == 0), stop=False)
                r_banks.append(r_ps)
            for half in range(2):
                r_ps = r_banks[half]
                for c in range(BLOCKS):
                    tokens = slice((2 * b + half) * P, (2 * b + half + 1) * P)
                    nc.tensor.matmul(
                        r_ps[:, c * P : (c + 1) * P], h32[:, c, tokens], ident32[:], is_transpose=True, start=False, stop=(c == BLOCKS - 1)
                    )
                stats = norm.tile([P, 6], F32, name="stats")
                nc.vector.bn_stats(stats[:], r_ps[:])
                nc.vector.bn_aggr(mean_var[:, half, :], stats[:])
            mean = mean_var[:, :, 0]
            rstd = norm.tile([P, 2], F32, name="rstd")
            neg_mean_rstd = norm.tile([P, 2], F32, name="neg_mean_rstd")
            if softmax_ended:
                nc.scalar.activation(rstd[:], mean_var[:, :, 1], ACT.Abs_reciprocal_sqrt, bias=eps[:])
                nc.vector.scalar_tensor_tensor(neg_mean_rstd[:], mean, -1.0, rstd[:], ALU.mult, ALU.mult)
            else:
                var_eps = norm.tile([P, 2], F32, name="var_eps")
                nc.vector.tensor_scalar_add(var_eps[:], mean_var[:, :, 1], EPS)
                neg_mean = norm.tile([P, 2], F32, name="neg_mean")
                nc.vector.tensor_scalar_mul(neg_mean[:], mean, -1.0)
                nc.gpsimd.tensor_tensor(rstd[:], var_eps[:], neg_half[:], ALU.pow)
                nc.gpsimd.tensor_tensor(neg_mean_rstd[:], neg_mean[:], rstd[:], ALU.mult)
            return r_banks, mean, rstd, neg_mean_rstd

        def centre(softmax_ended, r_banks, mean, rstd, neg_mean_rstd):
            normed = []
            for half in range(2):
                centred = norm.tile([P, D], F32, name="centred")
                column = slice(half, half + 1)
                if softmax_ended and half == 1:
                    nc.vector.tensor_scalar(centred[:], r_banks[half][:], mean[:, column], rstd[:, column], ALU.subtract, ALU.mult)
                else:
                    nc.scalar.activation(
                        centred[:], r_banks[half][:], ACT.Identity, bias=neg_mean_rstd[:, column], scale=rstd[:, column]
                    )
                normed.append(centred)
            return normed

        def finish(b, normed):
            back_banks = [new_bank("back_ps") for pair in range(BLOCKS // 2)]
            for half in range(2):
                for e in range(BLOCKS):
                    at = (e % 2) * T + half * P
                    nc.tensor.transpose(back_banks[e // 2][:, at : at + P], normed[half][:, e * P : (e + 1) * P], ident32[:])
            for pair in range(BLOCKS // 2):
                back_ps = back_banks[pair]
                y = leaving.tile([P, 2, T], F32, name="y")
                for i in range(2):
                    e = 2 * pair + i
                    gain, bias = gains[:, e : e + 1], biases[:, e : e + 1]
                    if pair == 0:
                        nc.scalar.activation(y[:, i, :], back_ps[:, i * T : (i + 1) * T], ACT.Identity, bias=bias, scale=gain)
                    else:
                        nc.vector.tensor_scalar(y[:, i, :], back_ps[:, i * T : (i + 1) * T], gain, bias, ALU.mult, ALU.add)
                nc.sync.dma_start(
                    out.rearrange("(e p) j -> p e j", p=P)[:, 2 * pair : 2 * pair + 2, b * T : (b + 1) * T], y[:]
                )

        def output_stage(x, softmax_ended):
            if x < SEQS:
                stats_of[x] = residual_stats(x, softmax_ended)
            if 0 <= x - 1 < SEQS:
                normed[x - 1] = centre(softmax_ended, *stats_of[x - 1])
            if 0 <= x - BACK < SEQS:
                finish(x - BACK, normed[x - BACK])

        for c in range(BLOCKS):
            for b in range(LEAD + 1):
                look_up(b, c)
        for b in range(LEAD + 1, SEQS):
            for c in range(BLOCKS):
                look_up(b, c)
        project_values(range(LEAD + 1))
        for b in range(LEAD):
            project(wq_sb, q16, b, 1)
            project(wk_sb, k16, b, 1)
        weights_of, stats_of, normed = {}, {}, {}
        for step in range(SEQS + 2 + BACK // 2):
            ahead = step + LEAD
            projecting = ahead < SEQS
            if not projecting and step <= SEQS:
                flipped = flip_weights(*weights_of[step - 1])
            if step < SEQS:
                raised = [exponentials(scores_ps) for scores_ps in scores(step)]
            if projecting:
                if step % 2 == 0:
                    project(wq_sb, q16, ahead, 2)
                else:
                    project(wk_sb, k16, ahead - 1, 2)
                if step >= 1:
                    flipped = flip_weights(*weights_of[step - 1])
            else:
                output_stage(2 * (ahead - SEQS) + 1, step >= SEQS)
                if step <= SEQS:
                    mix_values(step - 1, flipped)
            if ahead + 1 < SEQS:
                project_values([ahead + 1])
            else:
                output_stage(2 * (ahead + 1 - SEQS), step >= SEQS)
            if projecting and step >= 1:
                mix_values(step - 1, flipped)
            if step < SEQS:
                weights_of[step] = [normalised(powers, total) for powers, total in raised]
